import numpy as np
import ml_dtypes


def mxq(x, axis, fmt="e4m3"):
    dtype, down = {"e4m3": (ml_dtypes.float8_e4m3fn, 7), "e5m2": (ml_dtypes.float8_e5m2, 14)}[fmt]
    v = np.moveaxis(np.asarray(x, np.float32).astype(ml_dtypes.bfloat16).astype(np.float64), axis, -1)
    blocks = v.reshape(v.shape[:-1] + (-1, 32))
    amax = np.abs(blocks).max(-1, keepdims=True)
    byte = np.maximum(np.where(amax > 0, np.frexp(amax)[1] - 1 + 127, 0) - down, 1)
    scale = np.exp2(byte - 127.0)
    codes = (blocks / scale).astype(np.float32).astype(dtype).astype(np.float64)
    return np.moveaxis((codes * scale).reshape(v.shape), -1, axis)


WIDE = False


def mx_kscale(k):
    if not WIDE:
        return np.ones(k)
    levels = np.array([10, -10, 5, -5, 0])
    a = np.random.permutation(np.resize(levels, k // 512 * 4)).reshape(k // 512, 4)
    idx = np.arange(k)
    return np.exp2(a[idx // 512, idx % 128 // 32])


BF16 = ml_dtypes.bfloat16


def bf(x):
    return np.asarray(x, np.float32).astype(BF16)


def f64(x):
    return np.asarray(x).astype(np.float64)


B, L, S, T, Q, F, H, O = 8, 512, 16, 32, 1024, 1024, 1024, 768


def setup_inputs():
    s, u = mx_kscale(F), mx_kscale(F)
    return {"q": bf(np.random.standard_normal((B, L, H)) * 3.0),
            "src": bf(np.random.standard_normal((B, S, F)) * s),
            "trg": bf(np.random.standard_normal((B, T, F)) * u),
            "Ws": bf(np.random.standard_normal((F, H)) / np.sqrt(F) / s[:, None]),
            "b_s": bf(np.random.standard_normal(H) * 0.3),
            "Wt": bf(np.random.standard_normal((F, H)) / np.sqrt(F) / u[:, None]),
            "b_t": bf(np.random.standard_normal(H) * 0.3)}


def reference(q, src, trg, Ws, b_s, Wt, b_t):
    s_key = (mxq(f64(src), 2, "e4m3") @ mxq(f64(Ws), 0, "e4m3")) + f64(b_s)
    t_key = (mxq(f64(trg), 2, "e4m3") @ mxq(f64(Wt), 0, "e4m3")) + f64(b_t)
    rel_key = np.tanh(s_key[:, None, :, :] + t_key[:, :, None, :]).reshape(B, T * S, H)
    w = (mxq(f64(q), 2, "e4m3") @ mxq(rel_key, 2, "e4m3").transpose(0, 2, 1)) / np.sqrt(H)
    return w.reshape(B, L, T, S)

@@ -1,0 +1,333 @@
+from contextlib import ExitStack
+
+import concourse.mybir as mybir
+from concourse.masks import make_identity
+
+F32 = mybir.dt.float32
+BF16 = mybir.dt.bfloat16
+U32 = mybir.dt.uint32
+U8 = mybir.dt.uint8
+FP8X4 = mybir.dt.float8_e4m3fn_x4
+ACT = mybir.ActivationFunctionType
+ALU = mybir.AluOpType
+
+P = 128
+B, L, S, T, H, F = 8, 512, 16, 32, 1024, 1024
+FLOPS = 2 * B * L * S * T * H + 2 * B * (S + T) * F * H
+
+TG = 16
+TV = T - TG
+PIN = True
+EQ_ON_S = (1,)
+EO_ON_V = ((6, 1), (6, 3), (7, 1), (7, 3))
+
+
+def tile_dynamicattention4_pa_t_kernel(tc, q, src, trg, Ws, b_s, Wt, b_t, out):
+    nc = tc.nc
+    with ExitStack() as ctx:
+        keep = ctx.enter_context(tc.tile_pool(name="keep", bufs=1))
+        big = ctx.enter_context(tc.tile_pool(name="big", bufs=7))
+        wgp = ctx.enter_context(tc.tile_pool(name="wgp", bufs=4))
+        qgp = ctx.enter_context(tc.tile_pool(name="qgp", bufs=2))
+        prep = ctx.enter_context(tc.tile_pool(name="prep", bufs=4))
+        relp = ctx.enter_context(tc.tile_pool(name="relp", bufs=2))
+        osp = ctx.enter_context(tc.tile_pool(name="osp", bufs=2))
+        ps = ctx.enter_context(tc.psum_pool(name="ps", bufs=1))
+        if PIN:
+            ctx.enter_context(tc.manual_schedule())
+
+        warm = keep.tile([P, 2], F32, name="warm")
+        nc.vector.memset(warm[:], 0.0)
+        bias_sb = keep.tile([P, 256], BF16, name="bias_sb")
+        nc.vector.memset(bias_sb[:], 0.0)
+        nc.scalar.activation(out=warm[:, 1:2], in_=warm[:, 0:1], func=ACT.Tanh)
+        ident = keep.tile([P, P], F32, name="ident")
+        make_identity(nc, ident[:])
+
+        w_raw = []
+        w_views = []
+        for W in (Ws, Wt):
+            Wv = W.rearrange("(g p j) h -> g p j h", g=2, p=P, j=4)
+            for gf in range(2):
+                w_raw.append(big.tile([P, 4, H], BF16, name="w_raw", tag="big"))
+                w_views.append(Wv[gf])
+        nc.sync.dma_start(out=w_raw[0][:, :, 0:512], in_=w_views[0][:, :, 0:512])
+        nc.sync.dma_start(out=w_raw[0][:, :, 512:1024], in_=w_views[0][:, :, 512:1024])
+        src_sb = keep.tile([P, F], BF16, name="src_sb")
+        nc.sync.dma_start(out=src_sb[:], in_=src.flatten_outer_dims())
+        trg_sb = keep.tile([P, 2, F], BF16, name="trg_sb")
+        nc.sync.dma_start(
+            out=trg_sb[:], in_=trg.flatten_outer_dims().rearrange("(r p) f -> p r f", p=P)
+        )
+        nc.sync.dma_start(out=bias_sb[0:4, :], in_=b_s.rearrange("(r c) -> r c", r=4))
+        nc.sync.dma_start(out=bias_sb[4:8, :], in_=b_t.rearrange("(r c) -> r c", r=4))
+        for k in range(1, 4):
+            nc.sync.dma_start(out=w_raw[k][:], in_=w_views[k])
+        q_raw = []
+        for b in range(B):
+            qr = big.tile([P, 4, H], BF16, name="q_raw", tag="big")
+            nc.sync.dma_start(out=qr[:], in_=q[b].rearrange("(p c) h -> p c h", c=4))
+            q_raw.append(qr)
+
+        wc = [keep.tile([P, 2, H], U32, name="wc%d" % w, align_bytes=64) for w in range(2)]
+        ws = [keep.tile([P, 2, H], U8, name="ws%d" % w, align_bytes=64) for w in range(2)]
+        wgs = {}
+
+        def regroup(k, gh):
+            wg = wgp.tile([P, 2048], BF16, name="wg", align_bytes=64)
+            wgs[(k, gh)] = wg
+            dst = wg[:].rearrange("p (u e c j) -> p u e c j", u=2, e=2, j=4)
+            sv = w_raw[k][:, :, 512 * gh : 512 * (gh + 1)].rearrange(
+                "p j (u c e) -> p u e c j", u=2, e=2
+            )
+            nc.vector.tensor_copy(out=dst[:, 0], in_=sv[:, 0])
+            nc.scalar.copy(out=dst[:, 1], in_=sv[:, 1])
+
+        def quant_w(k, gh):
+            w, gf = divmod(k, 2)
+            nc.vector.quantize_mx(
+                out=wc[w][:, gf, 512 * gh : 512 * (gh + 1)].bitcast(FP8X4),
+                scales=ws[w][:, gf, 512 * gh : 512 * (gh + 1)],
+                in_=wgs[(k, gh)][:],
+            )
+
+        regroup(0, 0)
+        regroup(0, 1)
+
+        xg = keep.tile([P, 3, 1024], BF16, name="xg", align_bytes=64)
+        xc = keep.tile([P, 3, 256], U32, name="xc", align_bytes=64)
+        xs = keep.tile([P, 3, 256], U8, name="xs", align_bytes=64)
+        for r in range(3):
+            x32 = (src_sb[:] if r == 0 else trg_sb[:, r - 1, :]).bitcast(F32)
+            xt = ps.tile([P, 512], F32, name="xt%d" % (r % 2))
+            for g in range(2):
+                for u in range(2):
+                    k = 2 * g + u
+                    nc.tensor.transpose(
+                        xt[:, k * P : (k + 1) * P], x32[:, 256 * g + u : 256 * (g + 1) : 2], ident[:]
+                    )
+            nc.vector.tensor_copy(
+                out=xg[:, r, :].bitcast(F32).rearrange("p (g c u) -> p g c u", g=2, u=2),
+                in_=xt[:].rearrange("p (g u c) -> p g c u", g=2, u=2),
+            )
+        bt_ps = ps.tile([P, 512], F32, name="xt1")
+        nc.tensor.transpose(bt_ps[:, 0:P], bias_sb[:].bitcast(F32), ident[:])
+        bias8 = keep.tile([P, 8], F32, name="bias8")
+        nc.vector.tensor_copy(out=bias8[:], in_=bt_ps[:, 0:8])
+
+        regroup(1, 0)
+        regroup(1, 1)
+        quant_w(0, 0)
+        quant_w(0, 1)
+        for r in range(3):
+            nc.vector.quantize_mx(out=xc[:, r, :].bitcast(FP8X4), scales=xs[:, r, :], in_=xg[:, r, :])
+        bias16 = bias8[:].bitcast(BF16)
+        bsum = keep.tile([P, 8], F32, name="bsum")
+        nc.vector.tensor_tensor(out=bsum[:], in0=bias16[:, 0:8], in1=bias16[:, 8:16], op=ALU.add)
+        regroup(2, 0)
+        regroup(2, 1)
+        quant_w(1, 0)
+        quant_w(1, 1)
+        regroup(3, 0)
+        regroup(3, 1)
+        quant_w(2, 0)
+        quant_w(2, 1)
+
+        s_ps = [ps.tile([P, 512], F32, name="s_ps%d" % gh) for gh in range(2)]
+        s_sb = keep.tile([P, 2, P, 4], F32, name="s_sb")
+        t_sb = keep.tile([P, 2, 2 * P, 4], F32, name="t_sb")
+        t_ps = {}
+
+        def project(gh):
+            for r in range(3):
+                w = 0 if r == 0 else 1
+                if r == 0:
+                    bank = s_ps[gh]
+                else:
+                    bank = ps.tile([P, 512], F32, name="ob%d" % (2 * gh + r - 1))
+                    t_ps[(gh, r)] = bank
+                for j in range(4):
+                    cols = slice(512 * gh + P * j, 512 * gh + P * (j + 1))
+                    for gf in range(2):
+                        nc.tensor.matmul_mx(
+                            out=bank[:, P * j : P * (j + 1)],
+                            lhsT=wc[w][:, gf, cols].bitcast(FP8X4),
+                            lhsT_scale=ws[w][:, gf, cols],
+                            rhs=xc[:, r, P * gf : P * (gf + 1)].bitcast(FP8X4),
+                            rhs_scale=xs[:, r, P * gf : P * (gf + 1)],
+                            start=(gf == 0),
+                            stop=(gf == 1),
+                        )
+
+        def keys_out(gh):
+            for r in (1, 2):
+                nc.vector.tensor_tensor(
+                    out=t_sb[:, gh, P * (r - 1) : P * r, :],
+                    in0=t_ps[(gh, r)][:].rearrange("p (j c) -> p c j", j=4),
+                    in1=bsum[:, 4 * gh : 4 * gh + 4].unsqueeze(1).to_broadcast([P, P, 4]),
+                    op=ALU.add,
+                )
+            if TG > 0:
+                nc.vector.tensor_copy(
+                    out=s_sb[:, gh], in_=s_ps[gh][:].rearrange("p (j c) -> p c j", j=4)
+                )
+
+        xts, qgs, qcs, pres, rels, rcs, obs, osts = {}, {}, {}, {}, {}, {}, {}, {}
+
+        def q_transposes(b, k):
+            g, cp = divmod(k, 2)
+            q32 = q_raw[b][:].rearrange("p c h -> p (c h)").bitcast(F32).rearrange("p (c k) -> p c k", c=4)
+            xt = ps.tile([P, 512], F32, name="xt%d" % (k % 2))
+            xts[(b, k)] = xt
+            for u in range(2):
+                for c2 in range(2):
+                    m = 2 * u + c2
+                    nc.tensor.transpose(
+                        xt[:, m * P : (m + 1) * P],
+                        q32[:, 2 * cp + c2, 256 * g + P * u : 256 * g + P * (u + 1)],
+                        ident[:],
+                    )
+
+        def q_out(b, k, on_scalar):
+            g, cp = divmod(k, 2)
+            if k == 0:
+                qgs[b] = qgp.tile([P, 4096], BF16, name="qg", align_bytes=64)
+            qg32 = qgs[b][:].bitcast(F32).rearrange("p (g l u) -> p g l u", g=2, u=2)
+            o = qg32[:, g, 256 * cp : 256 * (cp + 1), :]
+            i = xts[(b, k)][:].rearrange("p (u l) -> p l u", u=2)
+            if on_scalar:
+                nc.scalar.copy(out=o, in_=i)
+            else:
+                nc.vector.tensor_copy(out=o, in_=i)
+
+        def q_quant(b):
+            qc = qgp.tile([P, 2, 512], U32, name="qc", align_bytes=64)
+            qs = qgp.tile([P, 2, 512], U8, name="qs", align_bytes=64)
+            qcs[b] = (qc, qs)
+            nc.vector.quantize_mx(
+                out=qc[:].rearrange("p g l -> p (g l)").bitcast(FP8X4),
+                scales=qs[:].rearrange("p g l -> p (g l)"),
+                in_=qgs[b][:],
+            )
+
+        def add(b, g):
+            pre = prep.tile([P, T, S, 4], F32, name="pre")
+            pres[(b, g)] = pre
+            nc.vector.tensor_tensor(
+                out=pre[:, 0:TV],
+                in0=s_ps[g][:]
+                .rearrange("p (j c) -> p c j", j=4)[:, S * b : S * (b + 1), :]
+                .unsqueeze(1)
+                .to_broadcast([P, TV, S, 4]),
+                in1=t_sb[:, g, T * b : T * b + TV, :].unsqueeze(2).to_broadcast([P, TV, S, 4]),
+                op=ALU.add,
+            )
+            if TG > 0:
+                nc.gpsimd.tensor_tensor(
+                    out=pre[:, TV:T],
+                    in0=s_sb[:, g, S * b : S * (b + 1), :].unsqueeze(1).to_broadcast([P, TG, S, 4]),
+                    in1=t_sb[:, g, T * b + TV : T * (b + 1), :].unsqueeze(2).to_broadcast([P, TG, S, 4]),
+                    op=ALU.add,
+                )
+
+        def tanh(b, g):
+            if g == 0:
+                rels[b] = relp.tile([P, 4096], BF16, name="rel", align_bytes=64)
+            nc.scalar.activation(
+                out=rels[b][:, 2048 * g : 2048 * (g + 1)],
+                in_=pres[(b, g)][:].rearrange("p t s j -> p (t s j)"),
+                func=ACT.Tanh,
+            )
+
+        def rel_quant(b):
+            rc = relp.tile([P, 2, 512], U32, name="rc", align_bytes=64)
+            rs = relp.tile([P, 2, 512], U8, name="rs", align_bytes=64)
+            rcs[b] = (rc, rs)
+            nc.vector.quantize_mx(
+                out=rc[:].rearrange("p g l -> p (g l)").bitcast(FP8X4),
+                scales=rs[:].rearrange("p g l -> p (g l)"),
+                in_=rels[b][:],
+            )
+
+        def scores(b, c):
+            qc, qs = qcs[b]
+            rc, rs = rcs[b]
+            ob = ps.tile([P, 512], F32, name="ob%d" % c)
+            obs[(b, c)] = ob
+            for g in range(2):
+                nc.tensor.matmul_mx(
+                    out=ob[:],
+                    lhsT=qc[:, g, P * c : P * (c + 1)].bitcast(FP8X4),
+                    lhsT_scale=qs[:, g, P * c : P * (c + 1)],
+                    rhs=rc[:, g, :].bitcast(FP8X4),
+                    rhs_scale=rs[:, g, :],
+                    start=(g == 0),
+                    stop=(g == 1),
+                )
+
+        def scores_out(b, c):
+            if c == 0:
+                osts[b] = osp.tile([P, 4, 512], F32, name="ost")
+            if (b, c) in EO_ON_V:
+                nc.vector.tensor_scalar_mul(out=osts[b][:, c, :], in0=obs[(b, c)][:], scalar1=1.0 / 32.0)
+            else:
+                nc.scalar.mul(out=osts[b][:, c, :], in_=obs[(b, c)][:], mul=1.0 / 32.0)
+            ov = out[b].rearrange("(p c) t s -> p c (t s)", c=4)
+            if b == B - 1:
+                nc.sync.dma_start(out=ov[:, c, :], in_=osts[b][:, c, :])
+            elif c == 3:
+                nc.sync.dma_start(out=ov, in_=osts[b][:])
+
+        quant_w(3, 0)
+        project(0)
+        quant_w(3, 1)
+        q_transposes(0, 0)
+        q_transposes(0, 1)
+        project(1)
+        keys_out(0)
+        q_out(0, 0, True)
+        q_out(0, 1, True)
+        q_transposes(0, 2)
+        q_transposes(0, 3)
+        add(0, 0)
+        keys_out(1)
+        q_out(0, 2, True)
+        q_out(0, 3, True)
+        add(0, 1)
+
+        for c in range(B + 2):
+            nxt, cur, mm, eo = c + 1, c, c - 1, c - 2
+            has_nxt, has_cur = nxt < B, cur < B
+            has_mm, has_eo = 0 <= mm < B, 0 <= eo < B
+            if has_nxt:
+                q_transposes(nxt, 0)
+                q_transposes(nxt, 1)
+                add(nxt, 0)
+            if has_cur:
+                tanh(cur, 0)
+            if has_mm:
+                rel_quant(mm)
+            if has_eo:
+                scores_out(eo, 0)
+                scores_out(eo, 1)
+            if has_mm:
+                scores(mm, 0)
+                scores(mm, 1)
+            if has_nxt:
+                q_out(nxt, 0, 0 in EQ_ON_S)
+                q_out(nxt, 1, 1 in EQ_ON_S)
+                q_transposes(nxt, 2)
+                q_transposes(nxt, 3)
+                add(nxt, 1)
+            if has_cur:
+                tanh(cur, 1)
+                q_quant(cur)
+            if has_eo:
+                scores_out(eo, 2)
+                scores_out(eo, 3)
+            if has_mm:
+                scores(mm, 2)
+                scores(mm, 3)
+            if has_nxt:
+                q_out(nxt, 2, 2 in EQ_ON_S)
+                q_out(nxt, 3, 3 in EQ_ON_S)

@@ -15,26 +15,25 @@ P = 128
 B, L, S, T, H, F = 8, 512, 16, 32, 1024, 1024
 FLOPS = 2 * B * L * S * T * H + 2 * B * (S + T) * F * H
 
-TG = 16
-TV = T - TG
-PIN = True
-EQ_ON_S = (1,)
-EO_ON_V = ((6, 1), (6, 3), (7, 1), (7, 3))
+
+def rows_g(b, g):
+    return {(0, 0): 8, (0, 1): 10}.get((b, g), 16)
 
 
 def tile_dynamicattention4_pa_t_kernel(tc, q, src, trg, Ws, b_s, Wt, b_t, out):
     nc = tc.nc
     with ExitStack() as ctx:
         keep = ctx.enter_context(tc.tile_pool(name="keep", bufs=1))
-        big = ctx.enter_context(tc.tile_pool(name="big", bufs=7))
+        big = ctx.enter_context(tc.tile_pool(name="big", bufs=6))
         wgp = ctx.enter_context(tc.tile_pool(name="wgp", bufs=4))
-        qgp = ctx.enter_context(tc.tile_pool(name="qgp", bufs=2))
+        qgp = ctx.enter_context(tc.tile_pool(name="qgp", bufs=4))
+        qcp = ctx.enter_context(tc.tile_pool(name="qcp", bufs=6))
         prep = ctx.enter_context(tc.tile_pool(name="prep", bufs=4))
-        relp = ctx.enter_context(tc.tile_pool(name="relp", bufs=2))
-        osp = ctx.enter_context(tc.tile_pool(name="osp", bufs=2))
+        relp = ctx.enter_context(tc.tile_pool(name="relp", bufs=3))
+        rcp = ctx.enter_context(tc.tile_pool(name="rcp", bufs=4))
+        osp = ctx.enter_context(tc.tile_pool(name="osp", bufs=3))
         ps = ctx.enter_context(tc.psum_pool(name="ps", bufs=1))
-        if PIN:
-            ctx.enter_context(tc.manual_schedule())
+        ctx.enter_context(tc.manual_schedule())
 
         warm = keep.tile([P, 2], F32, name="warm")
         nc.vector.memset(warm[:], 0.0)
@@ -44,44 +43,54 @@ def tile_dynamicattention4_pa_t_kernel(tc, q, src, trg, Ws, b_s, Wt, b_t, out):
         ident = keep.tile([P, P], F32, name="ident")
         make_identity(nc, ident[:])
 
-        w_raw = []
+        src_sb = keep.tile([P, F], BF16, name="src_sb")
+        trg_sb = keep.tile([P, 2, F], BF16, name="trg_sb")
+        xg = keep.tile([P, 3, 1024], BF16, name="xg", align_bytes=64)
+        xc = keep.tile([P, 3, 256], U32, name="xc", align_bytes=64)
+        xs = keep.tile([P, 3, 256], U8, name="xs", align_bytes=64)
+        bias8 = keep.tile([P, 8], F32, name="bias8")
+        bsum = keep.tile([P, 8], F32, name="bsum")
+        wc = [keep.tile([P, 2, H], U32, name="wc%d" % w, align_bytes=64) for w in range(2)]
+        ws = [keep.tile([P, 2, H], U8, name="ws%d" % w, align_bytes=64) for w in range(2)]
+        s_ps = [ps.tile([P, 512], F32, name="s_ps%d" % gh) for gh in range(2)]
+        s_sb = keep.tile([P, 2, P, 4], F32, name="s_sb")
+        t_sb = keep.tile([P, 2, 2 * P, 4], F32, name="t_sb")
         w_views = []
         for W in (Ws, Wt):
             Wv = W.rearrange("(g p j) h -> g p j h", g=2, p=P, j=4)
-            for gf in range(2):
-                w_raw.append(big.tile([P, 4, H], BF16, name="w_raw", tag="big"))
-                w_views.append(Wv[gf])
-        nc.sync.dma_start(out=w_raw[0][:, :, 0:512], in_=w_views[0][:, :, 0:512])
-        nc.sync.dma_start(out=w_raw[0][:, :, 512:1024], in_=w_views[0][:, :, 512:1024])
-        src_sb = keep.tile([P, F], BF16, name="src_sb")
-        nc.sync.dma_start(out=src_sb[:], in_=src.flatten_outer_dims())
-        trg_sb = keep.tile([P, 2, F], BF16, name="trg_sb")
-        nc.sync.dma_start(
-            out=trg_sb[:], in_=trg.flatten_outer_dims().rearrange("(r p) f -> p r f", p=P)
-        )
-        nc.sync.dma_start(out=bias_sb[0:4, :], in_=b_s.rearrange("(r c) -> r c", r=4))
-        nc.sync.dma_start(out=bias_sb[4:8, :], in_=b_t.rearrange("(r c) -> r c", r=4))
-        for k in range(1, 4):
-            nc.sync.dma_start(out=w_raw[k][:], in_=w_views[k])
-        q_raw = []
-        for b in range(B):
-            qr = big.tile([P, 4, H], BF16, name="q_raw", tag="big")
-            nc.sync.dma_start(out=qr[:], in_=q[b].rearrange("(p c) h -> p c h", c=4))
-            q_raw.append(qr)
+            w_views.extend([Wv[0], Wv[1]])
+        w_raw, q_raw, wgs, xts, t_ps = {}, {}, {}, {}, {}
+        qgs, qcs, pres, rels, rcs, obs, osts = {}, {}, {}, {}, {}, {}, {}
 
-        wc = [keep.tile([P, 2, H], U32, name="wc%d" % w, align_bytes=64) for w in range(2)]
-        ws = [keep.tile([P, 2, H], U8, name="ws%d" % w, align_bytes=64) for w in range(2)]
-        wgs = {}
+        def load_w(k, h):
+            if k not in w_raw:
+                w_raw[k] = big.tile([P, 2, 4, 512], BF16, name="w_raw", tag="big")
+            nc.sync.dma_start(out=w_raw[k][:, h], in_=w_views[k][:, :, 512 * h : 512 * (h + 1)])
 
-        def regroup(k, gh):
-            wg = wgp.tile([P, 2048], BF16, name="wg", align_bytes=64)
-            wgs[(k, gh)] = wg
-            dst = wg[:].rearrange("p (u e c j) -> p u e c j", u=2, e=2, j=4)
-            sv = w_raw[k][:, :, 512 * gh : 512 * (gh + 1)].rearrange(
-                "p j (u c e) -> p u e c j", u=2, e=2
+        def load_x():
+            nc.sync.dma_start(out=src_sb[:], in_=src.flatten_outer_dims())
+            nc.sync.dma_start(
+                out=trg_sb[:], in_=trg.flatten_outer_dims().rearrange("(r p) f -> p r f", p=P)
             )
-            nc.vector.tensor_copy(out=dst[:, 0], in_=sv[:, 0])
-            nc.scalar.copy(out=dst[:, 1], in_=sv[:, 1])
+            nc.sync.dma_start(out=bias_sb[0:4, :], in_=b_s.rearrange("(r c) -> r c", r=4))
+            nc.sync.dma_start(out=bias_sb[4:8, :], in_=b_t.rearrange("(r c) -> r c", r=4))
+
+        def load_q(b):
+            q_raw[b] = big.tile([P, 4, H], BF16, name="q_raw", tag="big")
+            nc.sync.dma_start(out=q_raw[b][:], in_=q[b].rearrange("(p c) h -> p c h", c=4))
+
+        def copy_on(on_scalar, o, i):
+            if on_scalar:
+                nc.scalar.copy(out=o, in_=i)
+            else:
+                nc.vector.tensor_copy(out=o, in_=i)
+
+        def regroup(k, gh, u, on_scalar):
+            if (k, gh) not in wgs:
+                wgs[(k, gh)] = wgp.tile([P, 2048], BF16, name="wg", align_bytes=64)
+            dst = wgs[(k, gh)][:].rearrange("p (u e c j) -> p u e c j", u=2, e=2, j=4)
+            sv = w_raw[k][:, gh].rearrange("p j (u c e) -> p u e c j", u=2, e=2)
+            copy_on(on_scalar, dst[:, u], sv[:, u])
 
         def quant_w(k, gh):
             w, gf = divmod(k, 2)
@@ -91,88 +100,105 @@ def tile_dynamicattention4_pa_t_kernel(tc, q, src, trg, Ws, b_s, Wt, b_t, out):
                 in_=wgs[(k, gh)][:],
             )
 
-        regroup(0, 0)
-        regroup(0, 1)
-
-        xg = keep.tile([P, 3, 1024], BF16, name="xg", align_bytes=64)
-        xc = keep.tile([P, 3, 256], U32, name="xc", align_bytes=64)
-        xs = keep.tile([P, 3, 256], U8, name="xs", align_bytes=64)
-        for r in range(3):
+        def x_transposes(r):
             x32 = (src_sb[:] if r == 0 else trg_sb[:, r - 1, :]).bitcast(F32)
             xt = ps.tile([P, 512], F32, name="xt%d" % (r % 2))
+            xts[("x", r)] = xt
             for g in range(2):
                 for u in range(2):
                     k = 2 * g + u
                     nc.tensor.transpose(
                         xt[:, k * P : (k + 1) * P], x32[:, 256 * g + u : 256 * (g + 1) : 2], ident[:]
                     )
-            nc.vector.tensor_copy(
-                out=xg[:, r, :].bitcast(F32).rearrange("p (g c u) -> p g c u", g=2, u=2),
-                in_=xt[:].rearrange("p (g u c) -> p g c u", g=2, u=2),
+
+        def x_out(r, on_scalar):
+            copy_on(
+                on_scalar,
+                xg[:, r, :].bitcast(F32).rearrange("p (g c u) -> p g c u", g=2, u=2),
+                xts[("x", r)][:].rearrange("p (g u c) -> p g c u", g=2, u=2),
             )
-        bt_ps = ps.tile([P, 512], F32, name="xt1")
-        nc.tensor.transpose(bt_ps[:, 0:P], bias_sb[:].bitcast(F32), ident[:])
-        bias8 = keep.tile([P, 8], F32, name="bias8")
-        nc.vector.tensor_copy(out=bias8[:], in_=bt_ps[:, 0:8])
 
-        regroup(1, 0)
-        regroup(1, 1)
-        quant_w(0, 0)
-        quant_w(0, 1)
-        for r in range(3):
-            nc.vector.quantize_mx(out=xc[:, r, :].bitcast(FP8X4), scales=xs[:, r, :], in_=xg[:, r, :])
-        bias16 = bias8[:].bitcast(BF16)
-        bsum = keep.tile([P, 8], F32, name="bsum")
-        nc.vector.tensor_tensor(out=bsum[:], in0=bias16[:, 0:8], in1=bias16[:, 8:16], op=ALU.add)
-        regroup(2, 0)
-        regroup(2, 1)
-        quant_w(1, 0)
-        quant_w(1, 1)
-        regroup(3, 0)
-        regroup(3, 1)
-        quant_w(2, 0)
-        quant_w(2, 1)
-
-        s_ps = [ps.tile([P, 512], F32, name="s_ps%d" % gh) for gh in range(2)]
-        s_sb = keep.tile([P, 2, P, 4], F32, name="s_sb")
-        t_sb = keep.tile([P, 2, 2 * P, 4], F32, name="t_sb")
-        t_ps = {}
-
-        def project(gh):
+        def x_quant():
             for r in range(3):
-                w = 0 if r == 0 else 1
-                if r == 0:
-                    bank = s_ps[gh]
-                else:
-                    bank = ps.tile([P, 512], F32, name="ob%d" % (2 * gh + r - 1))
-                    t_ps[(gh, r)] = bank
-                for j in range(4):
-                    cols = slice(512 * gh + P * j, 512 * gh + P * (j + 1))
-                    for gf in range(2):
-                        nc.tensor.matmul_mx(
-                            out=bank[:, P * j : P * (j + 1)],
-                            lhsT=wc[w][:, gf, cols].bitcast(FP8X4),
-                            lhsT_scale=ws[w][:, gf, cols],
-                            rhs=xc[:, r, P * gf : P * (gf + 1)].bitcast(FP8X4),
-                            rhs_scale=xs[:, r, P * gf : P * (gf + 1)],
-                            start=(gf == 0),
-                            stop=(gf == 1),
-                        )
+                nc.vector.quantize_mx(out=xc[:, r, :].bitcast(FP8X4), scales=xs[:, r, :], in_=xg[:, r, :])
 
-        def keys_out(gh):
-            for r in (1, 2):
-                nc.vector.tensor_tensor(
-                    out=t_sb[:, gh, P * (r - 1) : P * r, :],
-                    in0=t_ps[(gh, r)][:].rearrange("p (j c) -> p c j", j=4),
-                    in1=bsum[:, 4 * gh : 4 * gh + 4].unsqueeze(1).to_broadcast([P, P, 4]),
-                    op=ALU.add,
-                )
-            if TG > 0:
-                nc.vector.tensor_copy(
-                    out=s_sb[:, gh], in_=s_ps[gh][:].rearrange("p (j c) -> p c j", j=4)
-                )
+        def bias_transpose():
+            xts["b"] = ps.tile([P, 512], F32, name="xt1")
+            nc.tensor.transpose(xts["b"][:, 0:P], bias_sb[:].bitcast(F32), ident[:])
 
-        xts, qgs, qcs, pres, rels, rcs, obs, osts = {}, {}, {}, {}, {}, {}, {}, {}
+        def bias_out():
+            nc.vector.tensor_copy(out=bias8[:], in_=xts["b"][:, 0:8])
+            bias16 = bias8[:].bitcast(BF16)
+            nc.vector.tensor_tensor(out=bsum[:], in0=bias16[:, 0:8], in1=bias16[:, 8:16], op=ALU.add)
+
+        def project(gh, r):
+            w = 0 if r == 0 else 1
+            if r == 0:
+                bank = s_ps[gh]
+            else:
+                bank = ps.tile([P, 512], F32, name="ob%d" % (2 * gh + r - 1))
+                t_ps[(gh, r)] = bank
+            for j in range(4):
+                cols = slice(512 * gh + P * j, 512 * gh + P * (j + 1))
+                for gf in range(2):
+                    nc.tensor.matmul_mx(
+                        out=bank[:, P * j : P * (j + 1)],
+                        lhsT=wc[w][:, gf, cols].bitcast(FP8X4),
+                        lhsT_scale=ws[w][:, gf, cols],
+                        rhs=xc[:, r, P * gf : P * (gf + 1)].bitcast(FP8X4),
+                        rhs_scale=xs[:, r, P * gf : P * (gf + 1)],
+                        start=(gf == 0),
+                        stop=(gf == 1),
+                    )
+
+        def t_keys_out(gh, r):
+            nc.vector.tensor_tensor(
+                out=t_sb[:, gh, P * (r - 1) : P * r, :],
+                in0=t_ps[(gh, r)][:].rearrange("p (j c) -> p c j", j=4),
+                in1=bsum[:, 4 * gh : 4 * gh + 4].unsqueeze(1).to_broadcast([P, P, 4]),
+                op=ALU.add,
+            )
+
+        def s_keys_copy(gh):
+            nc.vector.tensor_copy(out=s_sb[:, gh], in_=s_ps[gh][:].rearrange("p (j c) -> p c j", j=4))
+
+        def pre_tile(b, g):
+            if (b, g) not in pres:
+                pres[(b, g)] = prep.tile([P, T, S, 4], F32, name="pre")
+            return pres[(b, g)]
+
+        def add_v(b, g):
+            tv = T - rows_g(b, g)
+            nc.vector.tensor_tensor(
+                out=pre_tile(b, g)[:, 0:tv],
+                in0=s_ps[g][:]
+                .rearrange("p (j c) -> p c j", j=4)[:, S * b : S * (b + 1), :]
+                .unsqueeze(1)
+                .to_broadcast([P, tv, S, 4]),
+                in1=t_sb[:, g, T * b : T * b + tv, :].unsqueeze(2).to_broadcast([P, tv, S, 4]),
+                op=ALU.add,
+            )
+
+        def add_g(b, g):
+            tg = rows_g(b, g)
+            nc.gpsimd.tensor_tensor(
+                out=pre_tile(b, g)[:, T - tg : T],
+                in0=s_sb[:, g, S * b : S * (b + 1), :].unsqueeze(1).to_broadcast([P, tg, S, 4]),
+                in1=t_sb[:, g, T * (b + 1) - tg : T * (b + 1), :].unsqueeze(2).to_broadcast([P, tg, S, 4]),
+                op=ALU.add,
+            )
+
+        def tanh(b, g):
+            rels[(b, g)] = relp.tile([P, 2048], BF16, name="rel", align_bytes=64)
+            nc.scalar.activation(
+                out=rels[(b, g)][:], in_=pres[(b, g)][:].rearrange("p t s j -> p (t s j)"), func=ACT.Tanh
+            )
+
+        def rel_quant(b, g):
+            rc = rcp.tile([P, 512], U32, name="rc", align_bytes=64)
+            rs = rcp.tile([P, 512], U8, name="rs", align_bytes=64)
+            rcs[(b, g)] = (rc, rs)
+            nc.vector.quantize_mx(out=rc[:].bitcast(FP8X4), scales=rs[:], in_=rels[(b, g)][:])
 
         def q_transposes(b, k):
             g, cp = divmod(k, 2)
@@ -190,144 +216,158 @@ def tile_dynamicattention4_pa_t_kernel(tc, q, src, trg, Ws, b_s, Wt, b_t, out):
 
         def q_out(b, k, on_scalar):
             g, cp = divmod(k, 2)
-            if k == 0:
-                qgs[b] = qgp.tile([P, 4096], BF16, name="qg", align_bytes=64)
-            qg32 = qgs[b][:].bitcast(F32).rearrange("p (g l u) -> p g l u", g=2, u=2)
-            o = qg32[:, g, 256 * cp : 256 * (cp + 1), :]
-            i = xts[(b, k)][:].rearrange("p (u l) -> p l u", u=2)
-            if on_scalar:
-                nc.scalar.copy(out=o, in_=i)
-            else:
-                nc.vector.tensor_copy(out=o, in_=i)
-
-        def q_quant(b):
-            qc = qgp.tile([P, 2, 512], U32, name="qc", align_bytes=64)
-            qs = qgp.tile([P, 2, 512], U8, name="qs", align_bytes=64)
-            qcs[b] = (qc, qs)
-            nc.vector.quantize_mx(
-                out=qc[:].rearrange("p g l -> p (g l)").bitcast(FP8X4),
-                scales=qs[:].rearrange("p g l -> p (g l)"),
-                in_=qgs[b][:],
+            if (b, g) not in qgs:
+                qgs[(b, g)] = qgp.tile([P, 2048], BF16, name="qg", align_bytes=64)
+            qg32 = qgs[(b, g)][:].bitcast(F32).rearrange("p (l u) -> p l u", u=2)
+            copy_on(
+                on_scalar,
+                qg32[:, 256 * cp : 256 * (cp + 1), :],
+                xts[(b, k)][:].rearrange("p (u l) -> p l u", u=2),
             )
 
-        def add(b, g):
-            pre = prep.tile([P, T, S, 4], F32, name="pre")
-            pres[(b, g)] = pre
-            nc.vector.tensor_tensor(
-                out=pre[:, 0:TV],
-                in0=s_ps[g][:]
-                .rearrange("p (j c) -> p c j", j=4)[:, S * b : S * (b + 1), :]
-                .unsqueeze(1)
-                .to_broadcast([P, TV, S, 4]),
-                in1=t_sb[:, g, T * b : T * b + TV, :].unsqueeze(2).to_broadcast([P, TV, S, 4]),
-                op=ALU.add,
-            )
-            if TG > 0:
-                nc.gpsimd.tensor_tensor(
-                    out=pre[:, TV:T],
-                    in0=s_sb[:, g, S * b : S * (b + 1), :].unsqueeze(1).to_broadcast([P, TG, S, 4]),
-                    in1=t_sb[:, g, T * b + TV : T * (b + 1), :].unsqueeze(2).to_broadcast([P, TG, S, 4]),
-                    op=ALU.add,
-                )
+        def q_quant(b, g):
+            qc = qcp.tile([P, 512], U32, name="qc", align_bytes=64)
+            qs = qcp.tile([P, 512], U8, name="qs", align_bytes=64)
+            qcs[(b, g)] = (qc, qs)
+            nc.vector.quantize_mx(out=qc[:].bitcast(FP8X4), scales=qs[:], in_=qgs[(b, g)][:])
 
-        def tanh(b, g):
+        def score_pass(b, c, g):
             if g == 0:
-                rels[b] = relp.tile([P, 4096], BF16, name="rel", align_bytes=64)
-            nc.scalar.activation(
-                out=rels[b][:, 2048 * g : 2048 * (g + 1)],
-                in_=pres[(b, g)][:].rearrange("p t s j -> p (t s j)"),
-                func=ACT.Tanh,
-            )
-
-        def rel_quant(b):
-            rc = relp.tile([P, 2, 512], U32, name="rc", align_bytes=64)
-            rs = relp.tile([P, 2, 512], U8, name="rs", align_bytes=64)
-            rcs[b] = (rc, rs)
-            nc.vector.quantize_mx(
-                out=rc[:].rearrange("p g l -> p (g l)").bitcast(FP8X4),
-                scales=rs[:].rearrange("p g l -> p (g l)"),
-                in_=rels[b][:],
+                obs[(b, c)] = ps.tile([P, 512], F32, name="ob%d" % c)
+            qc, qs = qcs[(b, g)]
+            rc, rs = rcs[(b, g)]
+            nc.tensor.matmul_mx(
+                out=obs[(b, c)][:],
+                lhsT=qc[:, P * c : P * (c + 1)].bitcast(FP8X4),
+                lhsT_scale=qs[:, P * c : P * (c + 1)],
+                rhs=rc[:].bitcast(FP8X4),
+                rhs_scale=rs[:],
+                start=(g == 0),
+                stop=(g == 1),
             )
 
         def scores(b, c):
-            qc, qs = qcs[b]
-            rc, rs = rcs[b]
-            ob = ps.tile([P, 512], F32, name="ob%d" % c)
-            obs[(b, c)] = ob
-            for g in range(2):
-                nc.tensor.matmul_mx(
-                    out=ob[:],
-                    lhsT=qc[:, g, P * c : P * (c + 1)].bitcast(FP8X4),
-                    lhsT_scale=qs[:, g, P * c : P * (c + 1)],
-                    rhs=rc[:, g, :].bitcast(FP8X4),
-                    rhs_scale=rs[:, g, :],
-                    start=(g == 0),
-                    stop=(g == 1),
-                )
+            score_pass(b, c, 0)
+            score_pass(b, c, 1)
 
-        def scores_out(b, c):
-            if c == 0:
+        def scores_out(b, c, on_scalar):
+            if b not in osts:
                 osts[b] = osp.tile([P, 4, 512], F32, name="ost")
-            if (b, c) in EO_ON_V:
-                nc.vector.tensor_scalar_mul(out=osts[b][:, c, :], in0=obs[(b, c)][:], scalar1=1.0 / 32.0)
-            else:
+            if on_scalar:
                 nc.scalar.mul(out=osts[b][:, c, :], in_=obs[(b, c)][:], mul=1.0 / 32.0)
+            else:
+                nc.vector.tensor_scalar_mul(out=osts[b][:, c, :], in0=obs[(b, c)][:], scalar1=1.0 / 32.0)
+
+        def store(b, c, n):
             ov = out[b].rearrange("(p c) t s -> p c (t s)", c=4)
-            if b == B - 1:
-                nc.sync.dma_start(out=ov[:, c, :], in_=osts[b][:, c, :])
-            elif c == 3:
-                nc.sync.dma_start(out=ov, in_=osts[b][:])
+            nc.sync.dma_start(out=ov[:, c : c + n, :], in_=osts[b][:, c : c + n, :])
 
-        quant_w(3, 0)
-        project(0)
+        def q_bank_on_scalar(b, k):
+            return b <= 1 or (b == 2 and k < 2)
+
+        def out_bank_on_scalar(b, c):
+            return b < 5 or c % 2 == 0
+
+        def q_pair_transposes(b, half):
+            q_transposes(b, 2 * half)
+            q_transposes(b, 2 * half + 1)
+
+        def q_pair_out(b, half):
+            q_out(b, 2 * half, q_bank_on_scalar(b, 2 * half))
+            q_out(b, 2 * half + 1, q_bank_on_scalar(b, 2 * half + 1))
+
+        def add(i):
+            add_v(i // 2, i % 2)
+            add_g(i // 2, i % 2)
+
+        def out_pair(b, half):
+            for c in (2 * half, 2 * half + 1):
+                scores_out(b, c, out_bank_on_scalar(b, c))
+                if b == B - 1:
+                    store(b, c, 1)
+            if b < B - 1:
+                store(b, 2 * half, 2)
+
+        load_w(0, 0)
+        load_x()
+        for k in range(1, 4):
+            load_w(k, 0)
+        for k in range(4):
+            load_w(k, 1)
+        load_q(0)
+        load_q(1)
+
+        for n in range(8):
+            gh, k = divmod(n, 4)
+            regroup(k, gh, 0, False)
+            regroup(k, gh, 1, True)
+            if n >= 4:
+                load_q(n - 2)
+            if n > 0:
+                quant_w((n - 1) % 4, (n - 1) // 4)
+            if n == 0:
+                for r in range(3):
+                    x_transposes(r)
+                    x_out(r, True)
+                bias_transpose()
+            if n == 1:
+                bias_out()
+                x_quant()
+            if n == 4:
+                for r in range(3):
+                    project(0, r)
+                s_keys_copy(0)
+            if n == 5:
+                t_keys_out(0, 1)
+                add(0)
+            if n == 6:
+                project(1, 0)
+            if n == 7:
+                tanh(0, 0)
         quant_w(3, 1)
-        q_transposes(0, 0)
-        q_transposes(0, 1)
-        project(1)
-        keys_out(0)
-        q_out(0, 0, True)
-        q_out(0, 1, True)
-        q_transposes(0, 2)
-        q_transposes(0, 3)
-        add(0, 0)
-        keys_out(1)
-        q_out(0, 2, True)
-        q_out(0, 3, True)
-        add(0, 1)
+        q_pair_transposes(0, 0)
+        project(1, 1)
+        project(1, 2)
+        q_pair_out(0, 0)
+        s_keys_copy(1)
+        t_keys_out(1, 1)
+        add(1)
+        q_pair_transposes(0, 1)
+        q_pair_out(0, 1)
+        load_q(6)
+        for half in range(2):
+            q_pair_transposes(1, half)
+            q_pair_out(1, half)
+        load_q(7)
+        t_keys_out(0, 2)
+        t_keys_out(1, 2)
+        q_quant(0, 0)
+        q_quant(0, 1)
 
-        for c in range(B + 2):
-            nxt, cur, mm, eo = c + 1, c, c - 1, c - 2
-            has_nxt, has_cur = nxt < B, cur < B
-            has_mm, has_eo = 0 <= mm < B, 0 <= eo < B
-            if has_nxt:
-                q_transposes(nxt, 0)
-                q_transposes(nxt, 1)
-                add(nxt, 0)
-            if has_cur:
-                tanh(cur, 0)
-            if has_mm:
-                rel_quant(mm)
-            if has_eo:
-                scores_out(eo, 0)
-                scores_out(eo, 1)
-            if has_mm:
-                scores(mm, 0)
-                scores(mm, 1)
-            if has_nxt:
-                q_out(nxt, 0, 0 in EQ_ON_S)
-                q_out(nxt, 1, 1 in EQ_ON_S)
-                q_transposes(nxt, 2)
-                q_transposes(nxt, 3)
-                add(nxt, 1)
-            if has_cur:
-                tanh(cur, 1)
-                q_quant(cur)
-            if has_eo:
-                scores_out(eo, 2)
-                scores_out(eo, 3)
-            if has_mm:
-                scores(mm, 2)
-                scores(mm, 3)
-            if has_nxt:
-                q_out(nxt, 2, 2 in EQ_ON_S)
-                q_out(nxt, 3, 3 in EQ_ON_S)
+        for i in range(2 * B + 5):
+            c, odd = divmod(i, 2)
+            qb = c + 2
+            if qb < B:
+                q_pair_transposes(qb, odd)
+            if 1 <= i <= 2 * B:
+                rel_quant((i - 1) // 2, (i - 1) % 2)
+            if i + 2 < 2 * B:
+                add(i + 2)
+            if qb < B and q_bank_on_scalar(qb, 2 * odd):
+                q_pair_out(qb, odd)
+            if 1 <= i < 2 * B:
+                tanh(c, odd)
+            if 0 <= c - 1 < B:
+                scores(c - 1, 2 * odd)
+                scores(c - 1, 2 * odd + 1)
+            eb = c - 1 if odd else c - 2
+            if 0 <= eb < B:
+                out_pair(eb, 1 - odd)
+            if qb < B and not q_bank_on_scalar(qb, 2 * odd):
+                q_pair_out(qb, odd)
+            if odd == 0 and c + 1 < B:
+                if c == 0:
+                    q_quant(1, 0)
+                q_quant(c + 1, 1)
+            if odd == 1 and c + 2 < B:
+                q_quant(c + 2, 0)

@@ -16,8 +16,11 @@ B, L, S, T, H, F = 8, 512, 16, 32, 1024, 1024
 FLOPS = 2 * B * L * S * T * H + 2 * B * (S + T) * F * H
 
 
+TILES = [(0, 0), (1, 0), (0, 1), (1, 1)] + [(b, g) for b in range(2, 8) for g in range(2)]
+
+
 def rows_g(b, g):
-    return {(0, 0): 8, (0, 1): 10}.get((b, g), 16)
+    return {(0, 0): 8, (0, 1): 10}.get((b, g), 12)
 
 
 def tile_dynamicattention4_pa_t_kernel(tc, q, src, trg, Ws, b_s, Wt, b_t, out):
@@ -159,8 +162,8 @@ def tile_dynamicattention4_pa_t_kernel(tc, q, src, trg, Ws, b_s, Wt, b_t, out):
                 op=ALU.add,
             )
 
-        def s_keys_copy(gh):
-            nc.vector.tensor_copy(out=s_sb[:, gh], in_=s_ps[gh][:].rearrange("p (j c) -> p c j", j=4))
+        def s_keys_copy(b, gh):
+            nc.vector.tensor_copy(out=s_sb[:, gh, S * b : S * (b + 1)], in_=s_ps[gh][:].rearrange("p (j c) -> p c j", j=4)[:, S * b : S * (b + 1)])
 
         def pre_tile(b, g):
             if (b, g) not in pres:
@@ -194,7 +197,8 @@ def tile_dynamicattention4_pa_t_kernel(tc, q, src, trg, Ws, b_s, Wt, b_t, out):
                 out=rels[(b, g)][:], in_=pres[(b, g)][:].rearrange("p t s j -> p (t s j)"), func=ACT.Tanh
             )
 
-        def rel_quant(b, g):
+        def rel_quant(i):
+            b, g = TILES[i]
             rc = rcp.tile([P, 512], U32, name="rc", align_bytes=64)
             rs = rcp.tile([P, 512], U8, name="rs", align_bytes=64)
             rcs[(b, g)] = (rc, rs)
@@ -233,7 +237,7 @@ def tile_dynamicattention4_pa_t_kernel(tc, q, src, trg, Ws, b_s, Wt, b_t, out):
 
         def score_pass(b, c, g):
             if g == 0:
-                obs[(b, c)] = ps.tile([P, 512], F32, name="ob%d" % c)
+                obs[(b, c)] = ps.tile([P, 512], F32, name=("xt0", "xt1", "s_ps0", "s_ps1")[c] if b == B - 1 else "ob%d" % c)
             qc, qs = qcs[(b, g)]
             rc, rs = rcs[(b, g)]
             nc.tensor.matmul_mx(
@@ -263,7 +267,7 @@ def tile_dynamicattention4_pa_t_kernel(tc, q, src, trg, Ws, b_s, Wt, b_t, out):
             nc.sync.dma_start(out=ov[:, c : c + n, :], in_=osts[b][:, c : c + n, :])
 
         def q_bank_on_scalar(b, k):
-            return b <= 1 or (b == 2 and k < 2)
+            return b <= 1 or k == 0
 
         def out_bank_on_scalar(b, c):
             return b < 5 or c % 2 == 0
@@ -277,8 +281,9 @@ def tile_dynamicattention4_pa_t_kernel(tc, q, src, trg, Ws, b_s, Wt, b_t, out):
             q_out(b, 2 * half + 1, q_bank_on_scalar(b, 2 * half + 1))
 
         def add(i):
-            add_v(i // 2, i % 2)
-            add_g(i // 2, i % 2)
+            s_keys_copy(*TILES[i])
+            add_g(*TILES[i])
+            add_v(*TILES[i])
 
         def out_pair(b, half):
             for c in (2 * half, 2 * half + 1):
@@ -316,7 +321,6 @@ def tile_dynamicattention4_pa_t_kernel(tc, q, src, trg, Ws, b_s, Wt, b_t, out):
             if n == 4:
                 for r in range(3):
                     project(0, r)
-                s_keys_copy(0)
             if n == 5:
                 t_keys_out(0, 1)
                 add(0)
@@ -326,48 +330,55 @@ def tile_dynamicattention4_pa_t_kernel(tc, q, src, trg, Ws, b_s, Wt, b_t, out):
                 tanh(0, 0)
         quant_w(3, 1)
         q_pair_transposes(0, 0)
+        add(1)
         project(1, 1)
         project(1, 2)
         q_pair_out(0, 0)
-        s_keys_copy(1)
+        tanh(1, 0)
         t_keys_out(1, 1)
-        add(1)
+        add(2)
         q_pair_transposes(0, 1)
         q_pair_out(0, 1)
         load_q(6)
-        for half in range(2):
-            q_pair_transposes(1, half)
-            q_pair_out(1, half)
-        load_q(7)
-        t_keys_out(0, 2)
-        t_keys_out(1, 2)
+        rel_quant(0)
+        tanh(0, 1)
+        q_pair_transposes(1, 0)
         q_quant(0, 0)
+        t_keys_out(0, 2)
+        q_pair_out(1, 0)
+        add(3)
+        t_keys_out(1, 2)
+        q_pair_transposes(1, 1)
+        rel_quant(1)
+        q_pair_out(1, 1)
+        load_q(7)
+        add(4)
         q_quant(0, 1)
+        q_quant(1, 0)
 
-        for i in range(2 * B + 5):
-            c, odd = divmod(i, 2)
-            qb = c + 2
-            if qb < B:
-                q_pair_transposes(qb, odd)
-            if 1 <= i <= 2 * B:
-                rel_quant((i - 1) // 2, (i - 1) % 2)
-            if i + 2 < 2 * B:
+        for i in range(3, 2 * B + 1):
+            if i + 1 < 2 * B:
+                q_pair_transposes(*divmod(i + 1, 2))
+            rel_quant(i - 1)
+            if i < 2 * B:
+                q_quant(*divmod(i, 2))
+            if 4 < i + 2 < 2 * B:
                 add(i + 2)
-            if qb < B and q_bank_on_scalar(qb, 2 * odd):
-                q_pair_out(qb, odd)
-            if 1 <= i < 2 * B:
-                tanh(c, odd)
-            if 0 <= c - 1 < B:
-                scores(c - 1, 2 * odd)
-                scores(c - 1, 2 * odd + 1)
-            eb = c - 1 if odd else c - 2
-            if 0 <= eb < B:
-                out_pair(eb, 1 - odd)
-            if qb < B and not q_bank_on_scalar(qb, 2 * odd):
-                q_pair_out(qb, odd)
-            if odd == 0 and c + 1 < B:
-                if c == 0:
-                    q_quant(1, 0)
-                q_quant(c + 1, 1)
-            if odd == 1 and c + 2 < B:
-                q_quant(c + 2, 0)
+            if i < 2 * B:
+                tanh(*TILES[i])
+            if i + 1 < 2 * B:
+                q_pair_out(*divmod(i + 1, 2))
+            if i == 2 * B:
+                for c in range(4):
+                    score_pass(B - 1, c, 1)
+                halves = [(B - 1, 0), (B - 1, 1)]
+            else:
+                halves = [(0, 0), (0, 1)] if i == 3 else [divmod(i - 2, 2)]
+                for b, half in halves:
+                    scores(b, 2 * half)
+                    scores(b, 2 * half + 1)
+                if i == 2 * B - 1:
+                    for c in range(4):
+                        score_pass(B - 1, c, 0)
+            for b, half in halves:
+                out_pair(b, half)

@@ -34,6 +34,7 @@ def tile_dynamicattention4_pa_t_kernel(tc, q, src, trg, Ws, b_s, Wt, b_t, out):
         prep = ctx.enter_context(tc.tile_pool(name="prep", bufs=4))
         relp = ctx.enter_context(tc.tile_pool(name="relp", bufs=3))
         rcp = ctx.enter_context(tc.tile_pool(name="rcp", bufs=4))
+        tgp = ctx.enter_context(tc.tile_pool(name="tgp", bufs=4))
         osp = ctx.enter_context(tc.tile_pool(name="osp", bufs=3))
         ps = ctx.enter_context(tc.psum_pool(name="ps", bufs=1))
         ctx.enter_context(tc.manual_schedule())
@@ -55,14 +56,12 @@ def tile_dynamicattention4_pa_t_kernel(tc, q, src, trg, Ws, b_s, Wt, b_t, out):
         bsum = keep.tile([P, 8], F32, name="bsum")
         wc = [keep.tile([P, 2, H], U32, name="wc%d" % w, align_bytes=64) for w in range(2)]
         ws = [keep.tile([P, 2, H], U8, name="ws%d" % w, align_bytes=64) for w in range(2)]
-        s_ps = [ps.tile([P, 512], F32, name="s_ps%d" % gh) for gh in range(2)]
         s_sb = keep.tile([P, 2, P, 4], F32, name="s_sb")
-        t_sb = keep.tile([P, 2, 2 * P, 4], F32, name="t_sb")
         w_views = []
         for W in (Ws, Wt):
             Wv = W.rearrange("(g p j) h -> g p j h", g=2, p=P, j=4)
             w_views.extend([Wv[0], Wv[1]])
-        w_raw, q_raw, wgs, xts, t_ps = {}, {}, {}, {}, {}
+        w_raw, q_raw, wgs, xts, k_ps, t_gs = {}, {}, {}, {}, {}, {}
         qgs, qcs, pres, rels, rcs, obs, osts = {}, {}, {}, {}, {}, {}, {}
 
         def load_w(k, h):
@@ -70,11 +69,13 @@ def tile_dynamicattention4_pa_t_kernel(tc, q, src, trg, Ws, b_s, Wt, b_t, out):
                 w_raw[k] = big.tile([P, 2, 4, 512], BF16, name="w_raw", tag="big")
             nc.sync.dma_start(out=w_raw[k][:, h], in_=w_views[k][:, :, 512 * h : 512 * (h + 1)])
 
-        def load_x():
+        def load_src():
             nc.sync.dma_start(out=src_sb[:], in_=src.flatten_outer_dims())
-            nc.sync.dma_start(
-                out=trg_sb[:], in_=trg.flatten_outer_dims().rearrange("(r p) f -> p r f", p=P)
-            )
+
+        def load_trg(r):
+            nc.sync.dma_start(out=trg_sb[:, r - 1], in_=trg.flatten_outer_dims()[P * (r - 1) : P * r])
+
+        def load_bias():
             nc.sync.dma_start(out=bias_sb[0:4, :], in_=b_s.rearrange("(r c) -> r c", r=4))
             nc.sync.dma_start(out=bias_sb[4:8, :], in_=b_t.rearrange("(r c) -> r c", r=4))
 
@@ -105,7 +106,7 @@ def tile_dynamicattention4_pa_t_kernel(tc, q, src, trg, Ws, b_s, Wt, b_t, out):
 
         def x_transposes(r):
             x32 = (src_sb[:] if r == 0 else trg_sb[:, r - 1, :]).bitcast(F32)
-            xt = ps.tile([P, 512], F32, name="xt%d" % (r % 2))
+            xt = ps.tile([P, 512], F32, name=("xt0", "xt1", "ob3")[r])
             xts[("x", r)] = xt
             for g in range(2):
                 for u in range(2):
@@ -121,9 +122,8 @@ def tile_dynamicattention4_pa_t_kernel(tc, q, src, trg, Ws, b_s, Wt, b_t, out):
                 xts[("x", r)][:].rearrange("p (g u c) -> p g c u", g=2, u=2),
             )
 
-        def x_quant():
-            for r in range(3):
-                nc.vector.quantize_mx(out=xc[:, r, :].bitcast(FP8X4), scales=xs[:, r, :], in_=xg[:, r, :])
+        def x_quant(r):
+            nc.vector.quantize_mx(out=xc[:, r, :].bitcast(FP8X4), scales=xs[:, r, :], in_=xg[:, r, :])
 
         def bias_transpose():
             xts["b"] = ps.tile([P, 512], F32, name="xt1")
@@ -136,11 +136,8 @@ def tile_dynamicattention4_pa_t_kernel(tc, q, src, trg, Ws, b_s, Wt, b_t, out):
 
         def project(gh, r):
             w = 0 if r == 0 else 1
-            if r == 0:
-                bank = s_ps[gh]
-            else:
-                bank = ps.tile([P, 512], F32, name="ob%d" % (2 * gh + r - 1))
-                t_ps[(gh, r)] = bank
+            bank = ps.tile([P, 512], F32, name=("ob%d" if r == 0 else "t_ps%d") % gh)
+            k_ps[(gh, min(r, 1))] = bank
             for j in range(4):
                 cols = slice(512 * gh + P * j, 512 * gh + P * (j + 1))
                 for gf in range(2):
@@ -154,16 +151,22 @@ def tile_dynamicattention4_pa_t_kernel(tc, q, src, trg, Ws, b_s, Wt, b_t, out):
                         stop=(gf == 1),
                     )
 
-        def t_keys_out(gh, r):
+        def s_keys_out(gh):
             nc.vector.tensor_tensor(
-                out=t_sb[:, gh, P * (r - 1) : P * r, :],
-                in0=t_ps[(gh, r)][:].rearrange("p (j c) -> p c j", j=4),
+                out=s_sb[:, gh],
+                in0=k_ps[(gh, 0)][:].rearrange("p (j c) -> p c j", j=4),
                 in1=bsum[:, 4 * gh : 4 * gh + 4].unsqueeze(1).to_broadcast([P, P, 4]),
                 op=ALU.add,
             )
 
-        def s_keys_copy(b, gh):
-            nc.vector.tensor_copy(out=s_sb[:, gh, S * b : S * (b + 1)], in_=s_ps[gh][:].rearrange("p (j c) -> p c j", j=4)[:, S * b : S * (b + 1)])
+        def t_keys(b, g, t0, t1):
+            c0 = T * (b % 4)
+            return k_ps[(g, 1)][:].rearrange("p (j c) -> p c j", j=4)[:, c0 + t0 : c0 + t1, :]
+
+        def t_slice(b, g):
+            tg = rows_g(b, g)
+            t_gs[(b, g)] = tgp.tile([P, tg, 4], F32, name="t_g", align_bytes=64)
+            nc.vector.tensor_copy(out=t_gs[(b, g)][:], in_=t_keys(b, g, T - tg, T))
 
         def pre_tile(b, g):
             if (b, g) not in pres:
@@ -174,11 +177,8 @@ def tile_dynamicattention4_pa_t_kernel(tc, q, src, trg, Ws, b_s, Wt, b_t, out):
             tv = T - rows_g(b, g)
             nc.vector.tensor_tensor(
                 out=pre_tile(b, g)[:, 0:tv],
-                in0=s_ps[g][:]
-                .rearrange("p (j c) -> p c j", j=4)[:, S * b : S * (b + 1), :]
-                .unsqueeze(1)
-                .to_broadcast([P, tv, S, 4]),
-                in1=t_sb[:, g, T * b : T * b + tv, :].unsqueeze(2).to_broadcast([P, tv, S, 4]),
+                in0=t_keys(b, g, 0, tv).unsqueeze(2).to_broadcast([P, tv, S, 4]),
+                in1=s_sb[:, g, S * b : S * (b + 1), :].unsqueeze(1).to_broadcast([P, tv, S, 4]),
                 op=ALU.add,
             )
 
@@ -187,22 +187,30 @@ def tile_dynamicattention4_pa_t_kernel(tc, q, src, trg, Ws, b_s, Wt, b_t, out):
             nc.gpsimd.tensor_tensor(
                 out=pre_tile(b, g)[:, T - tg : T],
                 in0=s_sb[:, g, S * b : S * (b + 1), :].unsqueeze(1).to_broadcast([P, tg, S, 4]),
-                in1=t_sb[:, g, T * (b + 1) - tg : T * (b + 1), :].unsqueeze(2).to_broadcast([P, tg, S, 4]),
+                in1=t_gs[(b, g)][:].unsqueeze(2).to_broadcast([P, tg, S, 4]),
                 op=ALU.add,
             )
 
-        def tanh(b, g):
-            rels[(b, g)] = relp.tile([P, 2048], BF16, name="rel", align_bytes=64)
+        def tanh(b, g, t0=0, t1=T):
+            if t0 == 0:
+                rels[(b, g)] = relp.tile([P, 2048], BF16, name="rel", align_bytes=64)
             nc.scalar.activation(
-                out=rels[(b, g)][:], in_=pres[(b, g)][:].rearrange("p t s j -> p (t s j)"), func=ACT.Tanh
+                out=rels[(b, g)][:, 64 * t0 : 64 * t1],
+                in_=pres[(b, g)][:, t0:t1].rearrange("p t s j -> p (t s j)"),
+                func=ACT.Tanh,
             )
 
-        def rel_quant(i):
+        def rel_quant(i, t0=0, t1=T):
             b, g = TILES[i]
-            rc = rcp.tile([P, 512], U32, name="rc", align_bytes=64)
-            rs = rcp.tile([P, 512], U8, name="rs", align_bytes=64)
-            rcs[(b, g)] = (rc, rs)
-            nc.vector.quantize_mx(out=rc[:].bitcast(FP8X4), scales=rs[:], in_=rels[(b, g)][:])
+            if t0 == 0:
+                rc = rcp.tile([P, 512], U32, name="rc", align_bytes=64)
+                rs = rcp.tile([P, 512], U8, name="rs", align_bytes=64)
+                rcs[(b, g)] = (rc, rs)
+            rc, rs = rcs[(b, g)]
+            cols = slice(S * t0, S * t1)
+            nc.vector.quantize_mx(
+                out=rc[:, cols].bitcast(FP8X4), scales=rs[:, cols], in_=rels[(b, g)][:, 64 * t0 : 64 * t1]
+            )
 
         def q_transposes(b, k):
             g, cp = divmod(k, 2)
@@ -235,17 +243,17 @@ def tile_dynamicattention4_pa_t_kernel(tc, q, src, trg, Ws, b_s, Wt, b_t, out):
             qcs[(b, g)] = (qc, qs)
             nc.vector.quantize_mx(out=qc[:].bitcast(FP8X4), scales=qs[:], in_=qgs[(b, g)][:])
 
-        def score_pass(b, c, g):
-            if g == 0:
-                obs[(b, c)] = ps.tile([P, 512], F32, name=("xt0", "xt1", "s_ps0", "s_ps1")[c] if b == B - 1 else "ob%d" % c)
+        def score_pass(b, c, g, n0=0, n1=512):
+            if g == 0 and n0 == 0:
+                obs[(b, c)] = ps.tile([P, 512], F32, name=("xt0", "xt1", "t_ps0", "t_ps1")[c] if b == B - 1 else "ob%d" % c)
             qc, qs = qcs[(b, g)]
             rc, rs = rcs[(b, g)]
             nc.tensor.matmul_mx(
-                out=obs[(b, c)][:],
+                out=obs[(b, c)][:, n0:n1],
                 lhsT=qc[:, P * c : P * (c + 1)].bitcast(FP8X4),
                 lhsT_scale=qs[:, P * c : P * (c + 1)],
-                rhs=rc[:].bitcast(FP8X4),
-                rhs_scale=rs[:],
+                rhs=rc[:, n0:n1].bitcast(FP8X4),
+                rhs_scale=rs[:, n0:n1],
                 start=(g == 0),
                 stop=(g == 1),
             )
@@ -254,17 +262,18 @@ def tile_dynamicattention4_pa_t_kernel(tc, q, src, trg, Ws, b_s, Wt, b_t, out):
             score_pass(b, c, 0)
             score_pass(b, c, 1)
 
-        def scores_out(b, c, on_scalar):
+        def scores_out(b, c, on_scalar, n0=0, n1=512):
             if b not in osts:
                 osts[b] = osp.tile([P, 4, 512], F32, name="ost")
+            o, i = osts[b][:, c, n0:n1], obs[(b, c)][:, n0:n1]
             if on_scalar:
-                nc.scalar.mul(out=osts[b][:, c, :], in_=obs[(b, c)][:], mul=1.0 / 32.0)
+                nc.scalar.mul(out=o, in_=i, mul=1.0 / 32.0)
             else:
-                nc.vector.tensor_scalar_mul(out=osts[b][:, c, :], in0=obs[(b, c)][:], scalar1=1.0 / 32.0)
+                nc.vector.tensor_scalar_mul(out=o, in0=i, scalar1=1.0 / 32.0)
 
-        def store(b, c, n):
+        def store(b, c, n, n0=0, n1=512):
             ov = out[b].rearrange("(p c) t s -> p c (t s)", c=4)
-            nc.sync.dma_start(out=ov[:, c : c + n, :], in_=osts[b][:, c : c + n, :])
+            nc.sync.dma_start(out=ov[:, c : c + n, n0:n1], in_=osts[b][:, c : c + n, n0:n1])
 
         def q_bank_on_scalar(b, k):
             return b <= 1 or k == 0
@@ -281,48 +290,73 @@ def tile_dynamicattention4_pa_t_kernel(tc, q, src, trg, Ws, b_s, Wt, b_t, out):
             q_out(b, 2 * half + 1, q_bank_on_scalar(b, 2 * half + 1))
 
         def add(i):
-            s_keys_copy(*TILES[i])
+            t_slice(*TILES[i])
             add_g(*TILES[i])
             add_v(*TILES[i])
 
         def out_pair(b, half):
             for c in (2 * half, 2 * half + 1):
                 scores_out(b, c, out_bank_on_scalar(b, c))
-                if b == B - 1:
-                    store(b, c, 1)
-            if b < B - 1:
-                store(b, 2 * half, 2)
+            store(b, 2 * half, 2)
+
+        def last_tile():
+            b, i = B - 1, 2 * B - 1
+            for h in range(2):
+                tanh(b, 1, 16 * h, 16 * (h + 1))
+            for c in (2, 3):
+                scores(b - 1, c)
+            for c in range(4):
+                score_pass(b, c, 0, 0, 256)
+            rel_quant(i, 0, 16)
+            for c in range(4):
+                score_pass(b, c, 1, 0, 256)
+            for c in range(4):
+                score_pass(b, c, 0, 256, 512)
+            rel_quant(i, 16, 32)
+            out_pair(b - 1, 1)
+            for c in range(4):
+                score_pass(b, c, 1, 256, 512)
+            for h in range(2):
+                for half in range(2):
+                    for c in (2 * half, 2 * half + 1):
+                        scores_out(b, c, c % 2 == 0, 256 * h, 256 * (h + 1))
+                    store(b, 2 * half, 2, 256 * h, 256 * (h + 1))
 
         load_w(0, 0)
-        load_x()
-        for k in range(1, 4):
+        load_src()
+        load_w(1, 0)
+        load_trg(1)
+        load_bias()
+        for k in range(2, 4):
             load_w(k, 0)
         for k in range(4):
             load_w(k, 1)
+        load_trg(2)
         load_q(0)
         load_q(1)
 
         for n in range(8):
             gh, k = divmod(n, 4)
-            regroup(k, gh, 0, False)
+            regroup(k, gh, 0, n == 7)
             regroup(k, gh, 1, True)
             if n >= 4:
                 load_q(n - 2)
             if n > 0:
                 quant_w((n - 1) % 4, (n - 1) // 4)
-            if n == 0:
-                for r in range(3):
-                    x_transposes(r)
-                    x_out(r, True)
-                bias_transpose()
+            if n in (0, 1):
+                x_transposes(n)
+                x_out(n, True)
             if n == 1:
+                bias_transpose()
+            if n in (1, 2):
+                x_quant(n - 1)
+            if n == 2:
                 bias_out()
-                x_quant()
             if n == 4:
-                for r in range(3):
-                    project(0, r)
+                project(0, 0)
+                project(0, 1)
             if n == 5:
-                t_keys_out(0, 1)
+                s_keys_out(0)
                 add(0)
             if n == 6:
                 project(1, 0)
@@ -330,24 +364,24 @@ def tile_dynamicattention4_pa_t_kernel(tc, q, src, trg, Ws, b_s, Wt, b_t, out):
                 tanh(0, 0)
         quant_w(3, 1)
         q_pair_transposes(0, 0)
+        x_transposes(2)
         add(1)
         project(1, 1)
-        project(1, 2)
+        s_keys_out(1)
         q_pair_out(0, 0)
         tanh(1, 0)
-        t_keys_out(1, 1)
+        x_out(2, True)
         add(2)
         q_pair_transposes(0, 1)
         q_pair_out(0, 1)
         load_q(6)
         rel_quant(0)
+        x_quant(2)
         tanh(0, 1)
         q_pair_transposes(1, 0)
         q_quant(0, 0)
-        t_keys_out(0, 2)
         q_pair_out(1, 0)
         add(3)
-        t_keys_out(1, 2)
         q_pair_transposes(1, 1)
         rel_quant(1)
         q_pair_out(1, 1)
@@ -356,29 +390,24 @@ def tile_dynamicattention4_pa_t_kernel(tc, q, src, trg, Ws, b_s, Wt, b_t, out):
         q_quant(0, 1)
         q_quant(1, 0)
 
-        for i in range(3, 2 * B + 1):
+        for i in range(3, 2 * B):
             if i + 1 < 2 * B:
                 q_pair_transposes(*divmod(i + 1, 2))
             rel_quant(i - 1)
-            if i < 2 * B:
-                q_quant(*divmod(i, 2))
+            q_quant(*divmod(i, 2))
             if 4 < i + 2 < 2 * B:
                 add(i + 2)
-            if i < 2 * B:
-                tanh(*TILES[i])
+            if i == 2 * B - 1:
+                last_tile()
+                continue
+            tanh(*TILES[i])
             if i + 1 < 2 * B:
                 q_pair_out(*divmod(i + 1, 2))
-            if i == 2 * B:
-                for c in range(4):
-                    score_pass(B - 1, c, 1)
-                halves = [(B - 1, 0), (B - 1, 1)]
-            else:
-                halves = [(0, 0), (0, 1)] if i == 3 else [divmod(i - 2, 2)]
-                for b, half in halves:
-                    scores(b, 2 * half)
-                    scores(b, 2 * half + 1)
-                if i == 2 * B - 1:
-                    for c in range(4):
-                        score_pass(B - 1, c, 0)
+            halves = [(0, 0), (0, 1)] if i == 3 else [divmod(i - 2, 2)]
+            for b, half in halves:
+                scores(b, 2 * half)
+                scores(b, 2 * half + 1)
+            if i in (4, 5):
+                project(i - 4, 2)
             for b, half in halves:
                 out_pair(b, half)

@@ -20,7 +20,7 @@ TILES = [(0, 0), (1, 0), (0, 1), (1, 1)] + [(b, g) for b in range(2, 8) for g in
 
 
 def rows_g(b, g):
-    return {(0, 0): 8, (0, 1): 10}.get((b, g), 12)
+    return {(0, 0): 8, (1, 0): 8}.get((b, g), 14 if g == 0 else 12)
 
 
 def tile_dynamicattention4_pa_t_kernel(tc, q, src, trg, Ws, b_s, Wt, b_t, out):
@@ -106,7 +106,7 @@ def tile_dynamicattention4_pa_t_kernel(tc, q, src, trg, Ws, b_s, Wt, b_t, out):
 
         def x_transposes(r):
             x32 = (src_sb[:] if r == 0 else trg_sb[:, r - 1, :]).bitcast(F32)
-            xt = ps.tile([P, 512], F32, name=("xt0", "xt1", "ob3")[r])
+            xt = ps.tile([P, 512], F32, name=("xt0", "xt1", "ob0")[r])
             xts[("x", r)] = xt
             for g in range(2):
                 for u in range(2):
@@ -215,7 +215,7 @@ def tile_dynamicattention4_pa_t_kernel(tc, q, src, trg, Ws, b_s, Wt, b_t, out):
         def q_transposes(b, k):
             g, cp = divmod(k, 2)
             q32 = q_raw[b][:].rearrange("p c h -> p (c h)").bitcast(F32).rearrange("p (c k) -> p c k", c=4)
-            xt = ps.tile([P, 512], F32, name="xt%d" % (k % 2))
+            xt = ps.tile([P, 512], F32, name=("xt0", "xt1", "ob2", "ob3")[k if b < 2 else k % 2])
             xts[(b, k)] = xt
             for u in range(2):
                 for c2 in range(2):
@@ -276,10 +276,10 @@ def tile_dynamicattention4_pa_t_kernel(tc, q, src, trg, Ws, b_s, Wt, b_t, out):
             nc.sync.dma_start(out=ov[:, c : c + n, n0:n1], in_=osts[b][:, c : c + n, n0:n1])
 
         def q_bank_on_scalar(b, k):
-            return b <= 1 or k == 0
+            return k == 0 if b > 1 else k % 2 == 1 or (b == 0 and k == 2)
 
         def out_bank_on_scalar(b, c):
-            return b < 5 or c % 2 == 0
+            return b < 5 or b == 6 or c % 2 == 0
 
         def q_pair_transposes(b, half):
             q_transposes(b, 2 * half)
@@ -301,8 +301,6 @@ def tile_dynamicattention4_pa_t_kernel(tc, q, src, trg, Ws, b_s, Wt, b_t, out):
 
         def last_tile():
             b, i = B - 1, 2 * B - 1
-            for h in range(2):
-                tanh(b, 1, 16 * h, 16 * (h + 1))
             for c in (2, 3):
                 scores(b - 1, c)
             for c in range(4):
@@ -363,48 +361,59 @@ def tile_dynamicattention4_pa_t_kernel(tc, q, src, trg, Ws, b_s, Wt, b_t, out):
             if n == 7:
                 tanh(0, 0)
         quant_w(3, 1)
-        q_pair_transposes(0, 0)
-        x_transposes(2)
         add(1)
+        tanh(1, 0)
         project(1, 1)
         s_keys_out(1)
-        q_pair_out(0, 0)
-        tanh(1, 0)
-        x_out(2, True)
-        add(2)
+        q_pair_transposes(0, 0)
         q_pair_transposes(0, 1)
+        x_transposes(2)
+        add(2)
+        q_pair_out(0, 0)
+        q_pair_transposes(1, 0)
+        rel_quant(0)
         q_pair_out(0, 1)
         load_q(6)
-        rel_quant(0)
-        x_quant(2)
         tanh(0, 1)
-        q_pair_transposes(1, 0)
-        q_quant(0, 0)
-        q_pair_out(1, 0)
-        add(3)
+        x_out(2, True)
         q_pair_transposes(1, 1)
         rel_quant(1)
-        q_pair_out(1, 1)
-        load_q(7)
-        add(4)
+        q_quant(0, 0)
+        add(3)
+        q_pair_out(1, 0)
         q_quant(0, 1)
+        tanh(1, 1)
+        q_pair_transposes(2, 0)
+        add(4)
+        q_pair_out(1, 1)
+        rel_quant(2)
+        for g in range(2):
+            for c in range(4):
+                score_pass(0, c, g)
+        load_q(7)
         q_quant(1, 0)
+        x_quant(2)
 
         for i in range(3, 2 * B):
-            if i + 1 < 2 * B:
+            if 3 < i < 2 * B - 1:
                 q_pair_transposes(*divmod(i + 1, 2))
-            rel_quant(i - 1)
+            if i > 3:
+                rel_quant(i - 1)
             q_quant(*divmod(i, 2))
             if 4 < i + 2 < 2 * B:
                 add(i + 2)
             if i == 2 * B - 1:
                 last_tile()
                 continue
-            tanh(*TILES[i])
+            if i > 3:
+                tanh(*TILES[i])
+            if i == 2 * B - 2:
+                for h in range(2):
+                    tanh(B - 1, 1, 16 * h, 16 * (h + 1))
             if i + 1 < 2 * B:
                 q_pair_out(*divmod(i + 1, 2))
             halves = [(0, 0), (0, 1)] if i == 3 else [divmod(i - 2, 2)]
-            for b, half in halves:
+            for b, half in halves if i > 3 else []:
                 scores(b, 2 * half)
                 scores(b, 2 * half + 1)
             if i in (4, 5):

@@ -92,8 +92,8 @@ def tile_dynamicattention4_pa_t_kernel(tc, q, src, trg, Ws, b_s, Wt, b_t, out):
         def regroup(k, gh, u, on_scalar):
             if (k, gh) not in wgs:
                 wgs[(k, gh)] = wgp.tile([P, 2048], BF16, name="wg", align_bytes=64)
-            dst = wgs[(k, gh)][:].rearrange("p (u e c j) -> p u e c j", u=2, e=2, j=4)
-            sv = w_raw[k][:, gh].rearrange("p j (u c e) -> p u e c j", u=2, e=2)
+            dst = wgs[(k, gh)][:].rearrange("p (u e c j) -> p u c j e", u=2, e=2, j=4)
+            sv = w_raw[k][:, gh].rearrange("p j (u c e) -> p u c j e", u=2, e=2)
             copy_on(on_scalar, dst[:, u], sv[:, u])
 
         def quant_w(k, gh):

@@ -29,8 +29,8 @@ def tile_dynamicattention4_pa_t_kernel(tc, q, src, trg, Ws, b_s, Wt, b_t, out):
         keep = ctx.enter_context(tc.tile_pool(name="keep", bufs=1))
         big = ctx.enter_context(tc.tile_pool(name="big", bufs=6))
         wgp = ctx.enter_context(tc.tile_pool(name="wgp", bufs=4))
-        qgp = ctx.enter_context(tc.tile_pool(name="qgp", bufs=4))
-        qcp = ctx.enter_context(tc.tile_pool(name="qcp", bufs=6))
+        qgp = ctx.enter_context(tc.tile_pool(name="qgp", bufs=2))
+        qcp = ctx.enter_context(tc.tile_pool(name="qcp", bufs=3))
         prep = ctx.enter_context(tc.tile_pool(name="prep", bufs=4))
         relp = ctx.enter_context(tc.tile_pool(name="relp", bufs=3))
         rcp = ctx.enter_context(tc.tile_pool(name="rcp", bufs=4))
@@ -131,6 +131,8 @@ def tile_dynamicattention4_pa_t_kernel(tc, q, src, trg, Ws, b_s, Wt, b_t, out):
 
         def bias_out():
             nc.vector.tensor_copy(out=bias8[:], in_=xts["b"][:, 0:8])
+
+        def bias_sum():
             bias16 = bias8[:].bitcast(BF16)
             nc.vector.tensor_tensor(out=bsum[:], in0=bias16[:, 0:8], in1=bias16[:, 8:16], op=ALU.add)
 
@@ -228,30 +230,33 @@ def tile_dynamicattention4_pa_t_kernel(tc, q, src, trg, Ws, b_s, Wt, b_t, out):
 
         def q_out(b, k, on_scalar):
             g, cp = divmod(k, 2)
-            if (b, g) not in qgs:
-                qgs[(b, g)] = qgp.tile([P, 2048], BF16, name="qg", align_bytes=64)
-            qg32 = qgs[(b, g)][:].bitcast(F32).rearrange("p (l u) -> p l u", u=2)
+            if b not in qgs:
+                qgs[b] = qgp.tile([P, 2, 2048], BF16, name="qg", align_bytes=64)
+            qg32 = qgs[b][:, g].bitcast(F32).rearrange("p (l u) -> p l u", u=2)
             copy_on(
                 on_scalar,
                 qg32[:, 256 * cp : 256 * (cp + 1), :],
                 xts[(b, k)][:].rearrange("p (u l) -> p l u", u=2),
             )
 
-        def q_quant(b, g):
-            qc = qcp.tile([P, 512], U32, name="qc", align_bytes=64)
-            qs = qcp.tile([P, 512], U8, name="qs", align_bytes=64)
-            qcs[(b, g)] = (qc, qs)
-            nc.vector.quantize_mx(out=qc[:].bitcast(FP8X4), scales=qs[:], in_=qgs[(b, g)][:])
+        def q_quant(b):
+            qc = qcp.tile([P, 1024], U32, name="qc", align_bytes=64)
+            qs = qcp.tile([P, 1024], U8, name="qs", align_bytes=64)
+            qcs[b] = (qc, qs)
+            nc.vector.quantize_mx(
+                out=qc[:].bitcast(FP8X4), scales=qs[:], in_=qgs[b][:].rearrange("p g n -> p (g n)")
+            )
 
         def score_pass(b, c, g, n0=0, n1=512):
             if g == 0 and n0 == 0:
                 obs[(b, c)] = ps.tile([P, 512], F32, name=("xt0", "xt1", "t_ps0", "t_ps1")[c] if b == B - 1 else "ob%d" % c)
-            qc, qs = qcs[(b, g)]
+            qc, qs = qcs[b]
+            cols = slice(512 * g + P * c, 512 * g + P * (c + 1))
             rc, rs = rcs[(b, g)]
             nc.tensor.matmul_mx(
                 out=obs[(b, c)][:, n0:n1],
-                lhsT=qc[:, P * c : P * (c + 1)].bitcast(FP8X4),
-                lhsT_scale=qs[:, P * c : P * (c + 1)],
+                lhsT=qc[:, cols].bitcast(FP8X4),
+                lhsT_scale=qs[:, cols],
                 rhs=rc[:, n0:n1].bitcast(FP8X4),
                 rhs_scale=rs[:, n0:n1],
                 start=(g == 0),
@@ -318,7 +323,8 @@ def tile_dynamicattention4_pa_t_kernel(tc, q, src, trg, Ws, b_s, Wt, b_t, out):
                 for half in range(2):
                     for c in (2 * half, 2 * half + 1):
                         scores_out(b, c, c % 2 == 0, 256 * h, 256 * (h + 1))
-                    store(b, 2 * half, 2, 256 * h, 256 * (h + 1))
+                    if h == 1:
+                        store(b, 2 * half, 2)
 
         load_w(0, 0)
         load_src()
@@ -350,6 +356,8 @@ def tile_dynamicattention4_pa_t_kernel(tc, q, src, trg, Ws, b_s, Wt, b_t, out):
                 x_quant(n - 1)
             if n == 2:
                 bias_out()
+            if n == 3:
+                bias_sum()
             if n == 4:
                 project(0, 0)
                 project(0, 1)
@@ -378,10 +386,9 @@ def tile_dynamicattention4_pa_t_kernel(tc, q, src, trg, Ws, b_s, Wt, b_t, out):
         x_out(2, True)
         q_pair_transposes(1, 1)
         rel_quant(1)
-        q_quant(0, 0)
         add(3)
         q_pair_out(1, 0)
-        q_quant(0, 1)
+        q_quant(0)
         tanh(1, 1)
         q_pair_transposes(2, 0)
         add(4)
@@ -391,7 +398,6 @@ def tile_dynamicattention4_pa_t_kernel(tc, q, src, trg, Ws, b_s, Wt, b_t, out):
             for c in range(4):
                 score_pass(0, c, g)
         load_q(7)
-        q_quant(1, 0)
         x_quant(2)
 
         for i in range(3, 2 * B):
@@ -399,7 +405,8 @@ def tile_dynamicattention4_pa_t_kernel(tc, q, src, trg, Ws, b_s, Wt, b_t, out):
                 q_pair_transposes(*divmod(i + 1, 2))
             if i > 3:
                 rel_quant(i - 1)
-            q_quant(*divmod(i, 2))
+            if i % 2 == 1:
+                q_quant(i // 2)
             if 4 < i + 2 < 2 * B:
                 add(i + 2)
             if i == 2 * B - 1:

@@ -29,8 +29,8 @@ def tile_dynamicattention4_pa_t_kernel(tc, q, src, trg, Ws, b_s, Wt, b_t, out):
         keep = ctx.enter_context(tc.tile_pool(name="keep", bufs=1))
         big = ctx.enter_context(tc.tile_pool(name="big", bufs=6))
         wgp = ctx.enter_context(tc.tile_pool(name="wgp", bufs=4))
-        qgp = ctx.enter_context(tc.tile_pool(name="qgp", bufs=2))
-        qcp = ctx.enter_context(tc.tile_pool(name="qcp", bufs=3))
+        qgp = ctx.enter_context(tc.tile_pool(name="qgp", bufs=4))
+        qcp = ctx.enter_context(tc.tile_pool(name="qcp", bufs=6))
         prep = ctx.enter_context(tc.tile_pool(name="prep", bufs=4))
         relp = ctx.enter_context(tc.tile_pool(name="relp", bufs=3))
         rcp = ctx.enter_context(tc.tile_pool(name="rcp", bufs=4))
@@ -230,33 +230,30 @@ def tile_dynamicattention4_pa_t_kernel(tc, q, src, trg, Ws, b_s, Wt, b_t, out):
 
         def q_out(b, k, on_scalar):
             g, cp = divmod(k, 2)
-            if b not in qgs:
-                qgs[b] = qgp.tile([P, 2, 2048], BF16, name="qg", align_bytes=64)
-            qg32 = qgs[b][:, g].bitcast(F32).rearrange("p (l u) -> p l u", u=2)
+            if (b, g) not in qgs:
+                qgs[(b, g)] = qgp.tile([P, 2048], BF16, name="qg", align_bytes=64)
+            qg32 = qgs[(b, g)][:].bitcast(F32).rearrange("p (l u) -> p l u", u=2)
             copy_on(
                 on_scalar,
                 qg32[:, 256 * cp : 256 * (cp + 1), :],
                 xts[(b, k)][:].rearrange("p (u l) -> p l u", u=2),
             )
 
-        def q_quant(b):
-            qc = qcp.tile([P, 1024], U32, name="qc", align_bytes=64)
-            qs = qcp.tile([P, 1024], U8, name="qs", align_bytes=64)
-            qcs[b] = (qc, qs)
-            nc.vector.quantize_mx(
-                out=qc[:].bitcast(FP8X4), scales=qs[:], in_=qgs[b][:].rearrange("p g n -> p (g n)")
-            )
+        def q_quant(b, g):
+            qc = qcp.tile([P, 512], U32, name="qc", align_bytes=64)
+            qs = qcp.tile([P, 512], U8, name="qs", align_bytes=64)
+            qcs[(b, g)] = (qc, qs)
+            nc.vector.quantize_mx(out=qc[:].bitcast(FP8X4), scales=qs[:], in_=qgs[(b, g)][:])
 
         def score_pass(b, c, g, n0=0, n1=512):
             if g == 0 and n0 == 0:
                 obs[(b, c)] = ps.tile([P, 512], F32, name=("xt0", "xt1", "t_ps0", "t_ps1")[c] if b == B - 1 else "ob%d" % c)
-            qc, qs = qcs[b]
-            cols = slice(512 * g + P * c, 512 * g + P * (c + 1))
+            qc, qs = qcs[(b, g)]
             rc, rs = rcs[(b, g)]
             nc.tensor.matmul_mx(
                 out=obs[(b, c)][:, n0:n1],
-                lhsT=qc[:, cols].bitcast(FP8X4),
-                lhsT_scale=qs[:, cols],
+                lhsT=qc[:, P * c : P * (c + 1)].bitcast(FP8X4),
+                lhsT_scale=qs[:, P * c : P * (c + 1)],
                 rhs=rc[:, n0:n1].bitcast(FP8X4),
                 rhs_scale=rs[:, n0:n1],
                 start=(g == 0),
@@ -386,9 +383,10 @@ def tile_dynamicattention4_pa_t_kernel(tc, q, src, trg, Ws, b_s, Wt, b_t, out):
         x_out(2, True)
         q_pair_transposes(1, 1)
         rel_quant(1)
+        q_quant(0, 0)
         add(3)
         q_pair_out(1, 0)
-        q_quant(0)
+        q_quant(0, 1)
         tanh(1, 1)
         q_pair_transposes(2, 0)
         add(4)
@@ -398,6 +396,7 @@ def tile_dynamicattention4_pa_t_kernel(tc, q, src, trg, Ws, b_s, Wt, b_t, out):
             for c in range(4):
                 score_pass(0, c, g)
         load_q(7)
+        q_quant(1, 0)
         x_quant(2)
 
         for i in range(3, 2 * B):
@@ -405,8 +404,7 @@ def tile_dynamicattention4_pa_t_kernel(tc, q, src, trg, Ws, b_s, Wt, b_t, out):
                 q_pair_transposes(*divmod(i + 1, 2))
             if i > 3:
                 rel_quant(i - 1)
-            if i % 2 == 1:
-                q_quant(i // 2)
+            q_quant(*divmod(i, 2))
             if 4 < i + 2 < 2 * B:
                 add(i + 2)
             if i == 2 * B - 1:

from contextlib import ExitStack

import concourse.mybir as mybir
from concourse.masks import make_identity

F32 = mybir.dt.float32
BF16 = mybir.dt.bfloat16
U32 = mybir.dt.uint32
U8 = mybir.dt.uint8
FP8X4 = mybir.dt.float8_e4m3fn_x4
ACT = mybir.ActivationFunctionType
ALU = mybir.AluOpType

P = 128
B, L, S, T, H, F = 8, 512, 16, 32, 1024, 1024
FLOPS = 2 * B * L * S * T * H + 2 * B * (S + T) * F * H


TILES = [(0, 0), (1, 0), (0, 1), (1, 1)] + [(b, g) for b in range(2, 8) for g in range(2)]


def rows_g(b, g):
    return {(0, 0): 8, (1, 0): 8}.get((b, g), 14 if g == 0 else 12)


def tile_dynamicattention4_pa_t_kernel(tc, q, src, trg, Ws, b_s, Wt, b_t, out):
    nc = tc.nc
    with ExitStack() as ctx:
        keep = ctx.enter_context(tc.tile_pool(name="keep", bufs=1))
        big = ctx.enter_context(tc.tile_pool(name="big", bufs=6))
        wgp = ctx.enter_context(tc.tile_pool(name="wgp", bufs=4))
        qgp = ctx.enter_context(tc.tile_pool(name="qgp", bufs=4))
        qcp = ctx.enter_context(tc.tile_pool(name="qcp", bufs=6))
        prep = ctx.enter_context(tc.tile_pool(name="prep", bufs=4))
        relp = ctx.enter_context(tc.tile_pool(name="relp", bufs=3))
        rcp = ctx.enter_context(tc.tile_pool(name="rcp", bufs=4))
        tgp = ctx.enter_context(tc.tile_pool(name="tgp", bufs=4))
        osp = ctx.enter_context(tc.tile_pool(name="osp", bufs=3))
        ps = ctx.enter_context(tc.psum_pool(name="ps", bufs=1))
        ctx.enter_context(tc.manual_schedule())

        warm = keep.tile([P, 2], F32, name="warm")
        nc.vector.memset(warm[:], 0.0)
        bias_sb = keep.tile([P, 256], BF16, name="bias_sb")
        nc.vector.memset(bias_sb[:], 0.0)
        nc.scalar.activation(out=warm[:, 1:2], in_=warm[:, 0:1], func=ACT.Tanh)
        ident = keep.tile([P, P], F32, name="ident")
        make_identity(nc, ident[:])

        src_sb = keep.tile([P, F], BF16, name="src_sb")
        trg_sb = keep.tile([P, 2, F], BF16, name="trg_sb")
        xg = keep.tile([P, 3, 1024], BF16, name="xg", align_bytes=64)
        xc = keep.tile([P, 3, 256], U32, name="xc", align_bytes=64)
        xs = keep.tile([P, 3, 256], U8, name="xs", align_bytes=64)
        bias8 = keep.tile([P, 8], F32, name="bias8")
        bsum = keep.tile([P, 8], F32, name="bsum")
        wc = [keep.tile([P, 2, H], U32, name="wc%d" % w, align_bytes=64) for w in range(2)]
        ws = [keep.tile([P, 2, H], U8, name="ws%d" % w, align_bytes=64) for w in range(2)]
        s_sb = keep.tile([P, 2, P, 4], F32, name="s_sb")
        w_views = []
        for W in (Ws, Wt):
            Wv = W.rearrange("(g p j) h -> g p j h", g=2, p=P, j=4)
            w_views.extend([Wv[0], Wv[1]])
        w_raw, q_raw, wgs, xts, k_ps, t_gs = {}, {}, {}, {}, {}, {}
        qgs, qcs, pres, rels, rcs, obs, osts = {}, {}, {}, {}, {}, {}, {}

        def load_w(k, h):
            if k not in w_raw:
                w_raw[k] = big.tile([P, 2, 4, 512], BF16, name="w_raw", tag="big")
            nc.sync.dma_start(out=w_raw[k][:, h], in_=w_views[k][:, :, 512 * h : 512 * (h + 1)])

        def load_src():
            nc.sync.dma_start(out=src_sb[:], in_=src.flatten_outer_dims())

        def load_trg(r):
            nc.sync.dma_start(out=trg_sb[:, r - 1], in_=trg.flatten_outer_dims()[P * (r - 1) : P * r])

        def load_bias():
            nc.sync.dma_start(out=bias_sb[0:4, :], in_=b_s.rearrange("(r c) -> r c", r=4))
            nc.sync.dma_start(out=bias_sb[4:8, :], in_=b_t.rearrange("(r c) -> r c", r=4))

        def load_q(b):
            q_raw[b] = big.tile([P, 4, H], BF16, name="q_raw", tag="big")
            nc.sync.dma_start(out=q_raw[b][:], in_=q[b].rearrange("(p c) h -> p c h", c=4))

        def copy_on(on_scalar, o, i):
            if on_scalar:
                nc.scalar.copy(out=o, in_=i)
            else:
                nc.vector.tensor_copy(out=o, in_=i)

        def regroup(k, gh, u, on_scalar):
            if (k, gh) not in wgs:
                wgs[(k, gh)] = wgp.tile([P, 2048], BF16, name="wg", align_bytes=64)
            dst = wgs[(k, gh)][:].rearrange("p (u e c j) -> p u c j e", u=2, e=2, j=4)
            sv = w_raw[k][:, gh].rearrange("p j (u c e) -> p u c j e", u=2, e=2)
            copy_on(on_scalar, dst[:, u], sv[:, u])

        def quant_w(k, gh):
            w, gf = divmod(k, 2)
            nc.vector.quantize_mx(
                out=wc[w][:, gf, 512 * gh : 512 * (gh + 1)].bitcast(FP8X4),
                scales=ws[w][:, gf, 512 * gh : 512 * (gh + 1)],
                in_=wgs[(k, gh)][:],
            )

        def x_transposes(r):
            x32 = (src_sb[:] if r == 0 else trg_sb[:, r - 1, :]).bitcast(F32)
            xt = ps.tile([P, 512], F32, name=("xt0", "xt1", "ob0")[r])
            xts[("x", r)] = xt
            for g in range(2):
                for u in range(2):
                    k = 2 * g + u
                    nc.tensor.transpose(
                        xt[:, k * P : (k + 1) * P], x32[:, 256 * g + u : 256 * (g + 1) : 2], ident[:]
                    )

        def x_out(r, on_scalar):
            copy_on(
                on_scalar,
                xg[:, r, :].bitcast(F32).rearrange("p (g c u) -> p g c u", g=2, u=2),
                xts[("x", r)][:].rearrange("p (g u c) -> p g c u", g=2, u=2),
            )

        def x_quant(r):
            nc.vector.quantize_mx(out=xc[:, r, :].bitcast(FP8X4), scales=xs[:, r, :], in_=xg[:, r, :])

        def bias_transpose():
            xts["b"] = ps.tile([P, 512], F32, name="xt1")
            nc.tensor.transpose(xts["b"][:, 0:P], bias_sb[:].bitcast(F32), ident[:])

        def bias_out():
            nc.vector.tensor_copy(out=bias8[:], in_=xts["b"][:, 0:8])

        def bias_sum():
            bias16 = bias8[:].bitcast(BF16)
            nc.vector.tensor_tensor(out=bsum[:], in0=bias16[:, 0:8], in1=bias16[:, 8:16], op=ALU.add)

        def project(gh, r):
            w = 0 if r == 0 else 1
            bank = ps.tile([P, 512], F32, name=("ob%d" if r == 0 else "t_ps%d") % gh)
            k_ps[(gh, min(r, 1))] = bank
            for j in range(4):
                cols = slice(512 * gh + P * j, 512 * gh + P * (j + 1))
                for gf in range(2):
                    nc.tensor.matmul_mx(
                        out=bank[:, P * j : P * (j + 1)],
                        lhsT=wc[w][:, gf, cols].bitcast(FP8X4),
                        lhsT_scale=ws[w][:, gf, cols],
                        rhs=xc[:, r, P * gf : P * (gf + 1)].bitcast(FP8X4),
                        rhs_scale=xs[:, r, P * gf : P * (gf + 1)],
                        start=(gf == 0),
                        stop=(gf == 1),
                    )

        def s_keys_out(gh):
            nc.vector.tensor_tensor(
                out=s_sb[:, gh],
                in0=k_ps[(gh, 0)][:].rearrange("p (j c) -> p c j", j=4),
                in1=bsum[:, 4 * gh : 4 * gh + 4].unsqueeze(1).to_broadcast([P, P, 4]),
                op=ALU.add,
            )

        def t_keys(b, g, t0, t1):
            c0 = T * (b % 4)
            return k_ps[(g, 1)][:].rearrange("p (j c) -> p c j", j=4)[:, c0 + t0 : c0 + t1, :]

        def t_slice(b, g):
            tg = rows_g(b, g)
            t_gs[(b, g)] = tgp.tile([P, tg, 4], F32, name="t_g", align_bytes=64)
            nc.vector.tensor_copy(out=t_gs[(b, g)][:], in_=t_keys(b, g, T - tg, T))

        def pre_tile(b, g):
            if (b, g) not in pres:
                pres[(b, g)] = prep.tile([P, T, S, 4], F32, name="pre")
            return pres[(b, g)]

        def add_v(b, g):
            tv = T - rows_g(b, g)
            nc.vector.tensor_tensor(
                out=pre_tile(b, g)[:, 0:tv],
                in0=t_keys(b, g, 0, tv).unsqueeze(2).to_broadcast([P, tv, S, 4]),
                in1=s_sb[:, g, S * b : S * (b + 1), :].unsqueeze(1).to_broadcast([P, tv, S, 4]),
                op=ALU.add,
            )

        def add_g(b, g):
            tg = rows_g(b, g)
            nc.gpsimd.tensor_tensor(
                out=pre_tile(b, g)[:, T - tg : T],
                in0=s_sb[:, g, S * b : S * (b + 1), :].unsqueeze(1).to_broadcast([P, tg, S, 4]),
                in1=t_gs[(b, g)][:].unsqueeze(2).to_broadcast([P, tg, S, 4]),
                op=ALU.add,
            )

        def tanh(b, g, t0=0, t1=T):
            if t0 == 0:
                rels[(b, g)] = relp.tile([P, 2048], BF16, name="rel", align_bytes=64)
            nc.scalar.activation(
                out=rels[(b, g)][:, 64 * t0 : 64 * t1],
                in_=pres[(b, g)][:, t0:t1].rearrange("p t s j -> p (t s j)"),
                func=ACT.Tanh,
            )

        def rel_quant(i, t0=0, t1=T):
            b, g = TILES[i]
            if t0 == 0:
                rc = rcp.tile([P, 512], U32, name="rc", align_bytes=64)
                rs = rcp.tile([P, 512], U8, name="rs", align_bytes=64)
                rcs[(b, g)] = (rc, rs)
            rc, rs = rcs[(b, g)]
            cols = slice(S * t0, S * t1)
            nc.vector.quantize_mx(
                out=rc[:, cols].bitcast(FP8X4), scales=rs[:, cols], in_=rels[(b, g)][:, 64 * t0 : 64 * t1]
            )

        def q_transposes(b, k):
            g, cp = divmod(k, 2)
            q32 = q_raw[b][:].rearrange("p c h -> p (c h)").bitcast(F32).rearrange("p (c k) -> p c k", c=4)
            xt = ps.tile([P, 512], F32, name=("xt0", "xt1", "ob2", "ob3")[k if b < 2 else k % 2])
            xts[(b, k)] = xt
            for u in range(2):
                for c2 in range(2):
                    m = 2 * u + c2
                    nc.tensor.transpose(
                        xt[:, m * P : (m + 1) * P],
                        q32[:, 2 * cp + c2, 256 * g + P * u : 256 * g + P * (u + 1)],
                        ident[:],
                    )

        def q_out(b, k, on_scalar):
            g, cp = divmod(k, 2)
            if (b, g) not in qgs:
                qgs[(b, g)] = qgp.tile([P, 2048], BF16, name="qg", align_bytes=64)
            qg32 = qgs[(b, g)][:].bitcast(F32).rearrange("p (l u) -> p l u", u=2)
            copy_on(
                on_scalar,
                qg32[:, 256 * cp : 256 * (cp + 1), :],
                xts[(b, k)][:].rearrange("p (u l) -> p l u", u=2),
            )

        def q_quant(b, g):
            qc = qcp.tile([P, 512], U32, name="qc", align_bytes=64)
            qs = qcp.tile([P, 512], U8, name="qs", align_bytes=64)
            qcs[(b, g)] = (qc, qs)
            nc.vector.quantize_mx(out=qc[:].bitcast(FP8X4), scales=qs[:], in_=qgs[(b, g)][:])

        def score_pass(b, c, g, n0=0, n1=512):
            if g == 0 and n0 == 0:
                obs[(b, c)] = ps.tile([P, 512], F32, name=("xt0", "xt1", "t_ps0", "t_ps1")[c] if b == B - 1 else "ob%d" % c)
            qc, qs = qcs[(b, g)]
            rc, rs = rcs[(b, g)]
            nc.tensor.matmul_mx(
                out=obs[(b, c)][:, n0:n1],
                lhsT=qc[:, P * c : P * (c + 1)].bitcast(FP8X4),
                lhsT_scale=qs[:, P * c : P * (c + 1)],
                rhs=rc[:, n0:n1].bitcast(FP8X4),
                rhs_scale=rs[:, n0:n1],
                start=(g == 0),
                stop=(g == 1),
            )

        def scores(b, c):
            score_pass(b, c, 0)
            score_pass(b, c, 1)

        def scores_out(b, c, on_scalar, n0=0, n1=512):
            if b not in osts:
                osts[b] = osp.tile([P, 4, 512], F32, name="ost")
            o, i = osts[b][:, c, n0:n1], obs[(b, c)][:, n0:n1]
            if on_scalar:
                nc.scalar.mul(out=o, in_=i, mul=1.0 / 32.0)
            else:
                nc.vector.tensor_scalar_mul(out=o, in0=i, scalar1=1.0 / 32.0)

        def store(b, c, n, n0=0, n1=512):
            ov = out[b].rearrange("(p c) t s -> p c (t s)", c=4)
            nc.sync.dma_start(out=ov[:, c : c + n, n0:n1], in_=osts[b][:, c : c + n, n0:n1])

        def q_bank_on_scalar(b, k):
            return k == 0 if b > 1 else k % 2 == 1 or (b == 0 and k == 2)

        def out_bank_on_scalar(b, c):
            return b < 5 or b == 6 or c % 2 == 0

        def q_pair_transposes(b, half):
            q_transposes(b, 2 * half)
            q_transposes(b, 2 * half + 1)

        def q_pair_out(b, half):
            q_out(b, 2 * half, q_bank_on_scalar(b, 2 * half))
            q_out(b, 2 * half + 1, q_bank_on_scalar(b, 2 * half + 1))

        def add(i):
            t_slice(*TILES[i])
            add_g(*TILES[i])
            add_v(*TILES[i])

        def out_pair(b, half):
            for c in (2 * half, 2 * half + 1):
                scores_out(b, c, out_bank_on_scalar(b, c))
            store(b, 2 * half, 2)

        def last_tile():
            b, i = B - 1, 2 * B - 1
            for c in (2, 3):
                scores(b - 1, c)
            for c in range(4):
                score_pass(b, c, 0, 0, 256)
            rel_quant(i, 0, 16)
            for c in range(4):
                score_pass(b, c, 1, 0, 256)
            for c in range(4):
                score_pass(b, c, 0, 256, 512)
            rel_quant(i, 16, 32)
            out_pair(b - 1, 1)
            for c in range(4):
                score_pass(b, c, 1, 256, 512)
            for h in range(2):
                for half in range(2):
                    for c in (2 * half, 2 * half + 1):
                        scores_out(b, c, c % 2 == 0, 256 * h, 256 * (h + 1))
                    if h == 1:
                        store(b, 2 * half, 2)

        load_w(0, 0)
        load_src()
        load_w(1, 0)
        load_trg(1)
        load_bias()
        for k in range(2, 4):
            load_w(k, 0)
        for k in range(4):
            load_w(k, 1)
        load_trg(2)
        load_q(0)
        load_q(1)

        for n in range(8):
            gh, k = divmod(n, 4)
            regroup(k, gh, 0, n == 7)
            regroup(k, gh, 1, True)
            if n >= 4:
                load_q(n - 2)
            if n > 0:
                quant_w((n - 1) % 4, (n - 1) // 4)
            if n in (0, 1):
                x_transposes(n)
                x_out(n, True)
            if n == 1:
                bias_transpose()
            if n in (1, 2):
                x_quant(n - 1)
            if n == 2:
                bias_out()
            if n == 3:
                bias_sum()
            if n == 4:
                project(0, 0)
                project(0, 1)
            if n == 5:
                s_keys_out(0)
                add(0)
            if n == 6:
                project(1, 0)
            if n == 7:
                tanh(0, 0)
        quant_w(3, 1)
        add(1)
        tanh(1, 0)
        project(1, 1)
        s_keys_out(1)
        q_pair_transposes(0, 0)
        q_pair_transposes(0, 1)
        x_transposes(2)
        add(2)
        q_pair_out(0, 0)
        q_pair_transposes(1, 0)
        rel_quant(0)
        q_pair_out(0, 1)
        load_q(6)
        tanh(0, 1)
        x_out(2, True)
        q_pair_transposes(1, 1)
        rel_quant(1)
        q_quant(0, 0)
        add(3)
        q_pair_out(1, 0)
        q_quant(0, 1)
        tanh(1, 1)
        q_pair_transposes(2, 0)
        add(4)
        q_pair_out(1, 1)
        rel_quant(2)
        for g in range(2):
            for c in range(4):
                score_pass(0, c, g)
        load_q(7)
        q_quant(1, 0)
        x_quant(2)

        for i in range(3, 2 * B):
            if 3 < i < 2 * B - 1:
                q_pair_transposes(*divmod(i + 1, 2))
            if i > 3:
                rel_quant(i - 1)
            q_quant(*divmod(i, 2))
            if 4 < i + 2 < 2 * B:
                add(i + 2)
            if i == 2 * B - 1:
                last_tile()
                continue
            if i > 3:
                tanh(*TILES[i])
            if i == 2 * B - 2:
                for h in range(2):
                    tanh(B - 1, 1, 16 * h, 16 * (h + 1))
            if i + 1 < 2 * B:
                q_pair_out(*divmod(i + 1, 2))
            halves = [(0, 0), (0, 1)] if i == 3 else [divmod(i - 2, 2)]
            for b, half in halves if i > 3 else []:
                scores(b, 2 * half)
                scores(b, 2 * half + 1)
            if i in (4, 5):
                project(i - 4, 2)
            for b, half in halves:
                out_pair(b, half)
